import numpy as np
import ml_dtypes


def mxq(x, axis, fmt="e4m3"):
    dtype, down = {"e4m3": (ml_dtypes.float8_e4m3fn, 7), "e5m2": (ml_dtypes.float8_e5m2, 14)}[fmt]
    v = np.moveaxis(np.asarray(x, np.float32).astype(ml_dtypes.bfloat16).astype(np.float64), axis, -1)
    blocks = v.reshape(v.shape[:-1] + (-1, 32))
    amax = np.abs(blocks).max(-1, keepdims=True)
    byte = np.maximum(np.where(amax > 0, np.frexp(amax)[1] - 1 + 127, 0) - down, 1)
    scale = np.exp2(byte - 127.0)
    codes = (blocks / scale).astype(np.float32).astype(dtype).astype(np.float64)
    return np.moveaxis((codes * scale).reshape(v.shape), -1, axis)


WIDE = False


def mx_kscale(k):
    if not WIDE:
        return np.ones(k)
    levels = np.array([10, -10, 5, -5, 0])
    a = np.random.permutation(np.resize(levels, k // 512 * 4)).reshape(k // 512, 4)
    idx = np.arange(k)
    return np.exp2(a[idx // 512, idx % 128 // 32])


BF16 = ml_dtypes.bfloat16


def bf(x):
    return np.asarray(x, np.float32).astype(BF16)


def f64(x):
    return np.asarray(x).astype(np.float64)


B, I, H = 1024, 1024, 1024
G = 2 * H
EPS = 1e-5


def ln(v):
    mu = v.mean(-1, keepdims=True)
    var = np.square(v - mu).mean(-1, keepdims=True)
    return (v - mu) / np.sqrt(var + EPS)


def sigmoid(v):
    return 1.0 / (1.0 + np.exp(-v))


def setup_inputs():
    s, t = mx_kscale(I), mx_kscale(H)
    return {"x": bf(np.random.standard_normal((B, I)) * s),
            "h": bf(np.random.standard_normal((B, H)) * t),
            "W_irz": bf(np.random.standard_normal((G, I)) / np.sqrt(I) / s),
            "b_irz": bf(np.random.standard_normal(G) * 0.5),
            "W_hrz": bf(np.random.standard_normal((G, H)) / np.sqrt(H) / t),
            "b_hrz": bf(np.random.standard_normal(G) * 0.5)}


def reference(x, h, W_irz, b_irz, W_hrz, b_hrz):
    i_rz = ln((mxq(f64(x), 1, "e4m3") @ mxq(f64(W_irz), 1, "e4m3").T) + f64(b_irz))
    h_rz = ln((mxq(f64(h), 1, "e4m3") @ mxq(f64(W_hrz), 1, "e4m3").T) + f64(b_hrz))
    return sigmoid(i_rz + h_rz)

@@ -1,0 +1,213 @@
+from contextlib import ExitStack
+
+import concourse.mybir as mybir
+from concourse.masks import make_identity
+
+F32 = mybir.dt.float32
+BF16 = mybir.dt.bfloat16
+U32 = mybir.dt.uint32
+U8 = mybir.dt.uint8
+FP8X4 = mybir.dt.float8_e4m3fn_x4
+ALU = mybir.AluOpType
+ACT = mybir.ActivationFunctionType
+
+P = 128
+B = 1024
+K = 1024
+G = 2048
+EPS = 1e-5
+NB = 512
+N_TILES = B // P
+N_BLOCKS = G // NB
+FLOPS = 2 * 2 * B * K * G
+
+V_COPY_EVERY = 8
+
+
+def tile_layernormgrucell_pa_kernel(tc, x, h, W_irz, b_irz, W_hrz, b_hrz, out):
+    nc = tc.nc
+    with ExitStack() as ctx:
+        const = ctx.enter_context(tc.tile_pool(name="const", bufs=1))
+        keep = ctx.enter_context(tc.tile_pool(name="keep", bufs=1))
+        rawp = ctx.enter_context(tc.tile_pool(name="rawp", bufs=5))
+        grp = ctx.enter_context(tc.tile_pool(name="grp", bufs=2))
+        vhp = ctx.enter_context(tc.tile_pool(name="vhp", bufs=3))
+        small = ctx.enter_context(tc.tile_pool(name="small", bufs=4))
+        ps_t = ctx.enter_context(tc.psum_pool(name="ps_t", bufs=4))
+        ps_a = ctx.enter_context(tc.psum_pool(name="ps_a", bufs=4))
+
+        ident = const.tile([P, P], F32, name="ident")
+        make_identity(nc, ident[:])
+        neghalf = const.tile([P, 1], F32, name="neghalf")
+        nc.gpsimd.memset(neghalf[:], -0.5)
+        poshalf = const.tile([P, 1], F32, name="poshalf")
+        nc.gpsimd.memset(poshalf[:], 0.5)
+        warm_in = const.tile([P, 1], F32, name="warm_in")
+        nc.vector.memset(warm_in[:], 0.0)
+        warm_out = const.tile([P, 1], F32, name="warm_out")
+        nc.scalar.activation(out=warm_out[:], in_=warm_in[:], func=ACT.Sigmoid)
+
+        bias = {}
+        codes = {}
+        planes = {}
+        for s in ("i", "h"):
+            bias[s] = const.tile([P, G], BF16, name="bias_%s" % s)
+            codes["w" + s] = keep.tile([P, N_BLOCKS, 2 * NB], U32, name="wc_%s" % s, align_bytes=64)
+            planes["w" + s] = keep.tile([P, N_BLOCKS, 2 * NB], U8, name="ws_%s" % s, align_bytes=64)
+            codes["a" + s] = keep.tile([P, 2, 2 * NB], U32, name="ac_%s" % s, align_bytes=64)
+            planes["a" + s] = keep.tile([P, 2, 2 * NB], U8, name="as_%s" % s, align_bytes=64)
+        v_i = [keep.tile([P, G], F32, name="v_i%d" % t) for t in range(N_TILES)]
+        junk = keep.tile([P, G], F32, name="junk")
+        part = {s: keep.tile([P, N_TILES, N_BLOCKS], F32, name="part_%s" % s) for s in ("i", "h")}
+        ssd = {s: keep.tile([P, N_TILES], F32, name="ssd_%s" % s) for s in ("i", "h")}
+        negmu = {s: keep.tile([P, N_TILES], F32, name="negmu_%s" % s) for s in ("i", "h")}
+        r_i = keep.tile([P, N_TILES], F32, name="r_i")
+        q_i = keep.tile([P, N_TILES], F32, name="q_i")
+
+        count = {"copies": 0}
+
+        def load(src_rows, pieces):
+            raw = rawp.tile([P, 4, K], BF16, name="raw")
+            view = src_rows.rearrange("(j p) k -> p j k", p=P)
+            if pieces == 1:
+                nc.sync.dma_start(out=raw[:], in_=view)
+            else:
+                for j in range(4):
+                    nc.sync.dma_start(out=raw[:, j, :], in_=view[:, j, :])
+            return raw
+
+        def prep(raw, kind, code_ap, plane_ap):
+            gq = grp.tile([P, 8 * NB], BF16, name="gq", align_bytes=64)
+            words = gq[:].bitcast(F32)
+            if kind == "w":
+                dest = words.rearrange("q (g n u) -> q g n u", g=2, n=NB, u=2)
+            else:
+                dest = words.rearrange("q (j g r u) -> q j g r u", j=4, g=2, r=P, u=2)
+            for j in range(4):
+                xt = ps_t.tile([P, 4, P], F32, name="xt")
+                rw = raw[:, j, :].bitcast(F32)
+                for s in range(4):
+                    nc.tensor.transpose(xt[:, s, :], rw[:, s * P:(s + 1) * P], ident[:])
+                src = xt[:].rearrange("q (g u) r -> q g r u", g=2, u=2)
+                if kind == "w":
+                    d = dest[:, :, j * P:(j + 1) * P, :]
+                else:
+                    d = dest[:, j, :, :, :]
+                count["copies"] += 1
+                if count["copies"] % V_COPY_EVERY == 0:
+                    nc.vector.tensor_copy(out=d, in_=src)
+                else:
+                    nc.scalar.copy(out=d, in_=src)
+            nc.vector.quantize_mx(out=code_ap.bitcast(FP8X4), scales=plane_ap, in_=gq[:])
+
+        def mx_bias(s, t, gb, v):
+            acc = ps_a.tile([P, NB], F32, name="acc")
+            grp_i, j = divmod(t, 4)
+            for g in range(2):
+                a0 = (j * 2 + g) * P
+                nc.tensor.matmul_mx(
+                    out=acc[:],
+                    lhsT=codes["a" + s][:, grp_i, a0:a0 + P].bitcast(FP8X4),
+                    lhsT_scale=planes["a" + s][:, grp_i, a0:a0 + P],
+                    rhs=codes["w" + s][:, gb, g * NB:(g + 1) * NB].bitcast(FP8X4),
+                    rhs_scale=planes["w" + s][:, gb, g * NB:(g + 1) * NB],
+                    start=(g == 0),
+                    stop=(g == 1),
+                )
+            cols = slice(gb * NB, (gb + 1) * NB)
+            nc.vector.scalar_tensor_tensor(
+                out=v[:, cols], in0=acc[:], scalar=1.0, in1=bias[s][:, cols],
+                op0=ALU.mult, op1=ALU.add, accum_out=part[s][:, t, gb:gb + 1],
+            )
+
+        def stats(s, t, v):
+            t2 = small.tile([P, 2], F32, name="t2")
+            nc.gpsimd.tensor_tensor(out=t2[:], in0=part[s][:, t, 0:2], in1=part[s][:, t, 2:4], op=ALU.add)
+            nc.gpsimd.tensor_scalar(
+                out=negmu[s][:, t:t + 1], in0=t2[:, 0:1], scalar1=t2[:, 1:2], scalar2=-1.0 / G,
+                op0=ALU.add, op1=ALU.mult,
+            )
+            nc.scalar.activation(
+                out=junk[:], in_=v[:], func=ACT.Square, bias=negmu[s][:, t:t + 1], scale=1.0,
+                accum_out=ssd[s][:, t:t + 1],
+            )
+            ve = small.tile([P, 1], F32, name="ve")
+            nc.gpsimd.tensor_scalar(
+                out=ve[:], in0=ssd[s][:, t:t + 1], scalar1=1.0 / G, scalar2=EPS,
+                op0=ALU.mult, op1=ALU.add,
+            )
+            return ve
+
+        raws = {}
+        raws["wi0"] = load(W_irz[0:NB, :], 4)
+        raws["ai0"] = load(x[0:NB, :], 1)
+        nc.sync.dma_start(out=bias["i"][:], in_=b_irz.partition_broadcast(P))
+
+        def prep_w(s, gb):
+            prep(raws["w%s%d" % (s, gb)], "w", codes["w" + s][:, gb, :], planes["w" + s][:, gb, :])
+
+        def prep_a(s, g2):
+            prep(raws["a%s%d" % (s, g2)], "a", codes["a" + s][:, g2, :], planes["a" + s][:, g2, :])
+
+        prep_w("i", 0)
+        raws["wi1"] = load(W_irz[NB:2 * NB, :], 1)
+        prep_a("i", 0)
+        raws["ai1"] = load(x[NB:2 * NB, :], 1)
+        for t in range(4):
+            mx_bias("i", t, 0, v_i[t])
+        prep_w("i", 1)
+        raws["wi2"] = load(W_irz[2 * NB:3 * NB, :], 1)
+        for t in range(4):
+            mx_bias("i", t, 1, v_i[t])
+        prep_a("i", 1)
+        raws["wi3"] = load(W_irz[3 * NB:4 * NB, :], 1)
+        for gb in range(2):
+            for t in range(4, 8):
+                mx_bias("i", t, gb, v_i[t])
+        prep_w("i", 2)
+        raws["ah0"] = load(h[0:NB, :], 1)
+        for t in range(N_TILES):
+            mx_bias("i", t, 2, v_i[t])
+        prep_w("i", 3)
+        raws["wh0"] = load(W_hrz[0:NB, :], 1)
+        nc.sync.dma_start(out=bias["h"][:], in_=b_hrz.partition_broadcast(P))
+        for t in range(N_TILES):
+            mx_bias("i", t, 3, v_i[t])
+            ve = stats("i", t, v_i[t])
+            nc.gpsimd.tensor_tensor(out=r_i[:, t:t + 1], in0=ve[:], in1=neghalf[:], op=ALU.pow)
+            nc.gpsimd.tensor_tensor(out=q_i[:, t:t + 1], in0=ve[:], in1=poshalf[:], op=ALU.pow)
+
+        prep_a("h", 0)
+        raws["ah1"] = load(h[NB:2 * NB, :], 1)
+        prep_w("h", 0)
+        raws["wh1"] = load(W_hrz[NB:2 * NB, :], 1)
+        prep_a("h", 1)
+        raws["wh2"] = load(W_hrz[2 * NB:3 * NB, :], 1)
+        prep_w("h", 1)
+        raws["wh3"] = load(W_hrz[3 * NB:4 * NB, :], 1)
+        prep_w("h", 2)
+        prep_w("h", 3)
+
+        for t in range(N_TILES):
+            v_h = vhp.tile([P, G], F32, name="v_h")
+            for gb in range(N_BLOCKS):
+                mx_bias("h", t, gb, v_h)
+            ve = stats("h", t, v_h)
+            r_h = small.tile([P, 1], F32, name="r_h")
+            nc.gpsimd.tensor_tensor(out=r_h[:], in0=ve[:], in1=neghalf[:], op=ALU.pow)
+            ratio = small.tile([P, 1], F32, name="ratio")
+            nc.gpsimd.tensor_tensor(out=ratio[:], in0=r_h[:], in1=q_i[:, t:t + 1], op=ALU.mult)
+            nc.vector.scalar_tensor_tensor(
+                out=v_h[:], in0=v_h[:], scalar=ratio[:], in1=v_i[t][:], op0=ALU.mult, op1=ALU.add,
+            )
+            shift = small.tile([P, 1], F32, name="shift")
+            nc.gpsimd.tensor_scalar(
+                out=shift[:], in0=negmu["h"][:, t:t + 1], scalar1=ratio[:], scalar2=negmu["i"][:, t:t + 1],
+                op0=ALU.mult, op1=ALU.add,
+            )
+            cbias = small.tile([P, 1], F32, name="cbias")
+            nc.gpsimd.tensor_tensor(out=cbias[:], in0=shift[:], in1=r_i[:, t:t + 1], op=ALU.mult)
+            nc.scalar.activation(
+                out=v_h[:], in_=v_h[:], func=ACT.Sigmoid, bias=cbias[:], scale=r_i[:, t:t + 1],
+            )
+            nc.sync.dma_start(out=out[t * P:(t + 1) * P, :], in_=v_h[:])

@@ -21,7 +21,71 @@ N_TILES = B // P
 N_BLOCKS = G // NB
 FLOPS = 2 * 2 * B * K * G
 
-V_COPY_EVERY = 8
+RAW_BUFS = 16
+GQ_BUFS = 3
+GA_BUFS = 6
+V_BUFS = 11
+PS_T = 4
+PS_A = 4
+LOAD_ORDER = ("wi0", "ai0.0", "ai0.1", "bi0", "wi1", "bi1", "wi2", "bi2", "wi3", "bi3", "ai0.2", "ai0.3", "ai1.0", "ai1.1", "ai1.2", "ai1.3", "wh0", "ah0.0", "ah0.1", "bh0", "wh1", "bh1", "wh2", "bh2", "wh3", "bh3", "ah0.2", "ah0.3", "ah1.0", "ah1.1", "ah1.2", "ah1.3")
+V_COPIES = frozenset((("ah0", 3), ("wh0", 3), ("ah1", 3), ("wh1", 3), ("wh2", 3), ("wh3", 3)))
+G_COMBINES = frozenset(())
+D_SPLIT = {7: 4}
+ORDER = (
+    "L.wi0.0", "L.wi0.1", "L.wi0.2", "L.wi0.3", "L.ai0.0", "L.ai0.1", "L.bi0", "L.wi1.0",
+    "L.wi1.1", "T.wi0.0", "L.wi1.2", "T.wi0.1", "L.wi1.3", "T.wi0.2", "P.wi0.1", "L.bi1",
+    "P.wi0.0", "T.wi0.3", "P.wi0.2", "L.wi2.0", "P.wi0.3", "L.wi2.1", "T.ai0.1", "L.wi2.2",
+    "T.ai0.0", "Q.wi0", "P.ai0.1", "L.wi2.3", "T.wi1.0", "P.ai0.0", "L.bi2", "T.wi1.1",
+    "P.wi1.0", "Q.ai0.0", "L.wi3.0", "Q.ai0.1", "T.wi1.2", "P.wi1.1", "L.wi3.1", "T.wi1.3",
+    "P.wi1.2", "L.wi3.2", "M.i.1.0", "P.wi1.3", "L.wi3.3", "M.i.0.0", "Q.wi1", "L.bi3",
+    "T.wi2.0", "T.wi2.1", "L.ai0.2", "P.wi2.0", "T.wi2.2", "A.i.0.0", "L.ai0.3", "T.wi2.3",
+    "P.wi2.2", "A.i.1.0", "L.ai1.0", "M.i.0.1", "P.wi2.3", "L.ai1.1", "M.i.1.1", "P.wi2.1",
+    "L.ai1.2", "T.wi3.0", "Q.wi2", "T.wi3.1", "L.ai1.3", "P.wi3.0", "T.wi3.2", "L.wh0.0",
+    "T.wi3.3", "P.wi3.1", "A.i.1.1", "L.wh0.1", "P.wi3.2", "M.i.0.2", "A.i.0.1", "L.wh0.2",
+    "P.wi3.3", "T.ai0.2", "L.wh0.3", "T.ai0.3", "Q.wi3", "P.ai0.2", "L.ah0.0", "T.ai1.0",
+    "P.ai0.3", "L.ah0.1", "T.ai1.1", "Q.ai0.2", "P.ai1.0", "A.i.0.2", "L.bh0", "T.ai1.2",
+    "M.i.0.3", "Q.ai0.3", "L.wh1.0", "P.ai1.2", "Q.ai1.0", "M.i.1.3", "L.wh1.1", "P.ai1.1",
+    "A.i.0.3", "M.i.2.1", "L.wh1.2", "A.i.1.3", "M.i.2.0", "L.wh1.3", "Q.ai1.1", "T.wh0.0",
+    "A.i.2.1", "L.bh1", "T.wh0.3", "P.wh0.0", "T.ai1.3", "L.wh2.0", "P.wh0.3", "T.wh0.1",
+    "N.i.0", "P.ai1.3", "T.wh0.2", "L.wh2.1", "A.i.2.0", "T.ah0.0", "L.wh2.2", "P.wh0.1",
+    "M.i.2.2", "Q.ai1.2", "P.wh0.2", "L.wh2.3", "Q.ai1.3", "M.i.3.0", "P.ah0.0", "A.i.2.2",
+    "L.bh2", "M.i.2.3", "B.i.0", "A.i.3.0", "L.wh3.0", "T.ah0.1", "A.i.2.3", "T.wh1.0",
+    "L.wh3.1", "T.wh1.3", "L.wh3.2", "Q.wh0", "T.wh1.1", "M.i.4.2", "L.wh3.3", "P.wh1.0",
+    "L.bh3", "M.i.4.1", "P.wh1.3", "P.wh1.1", "M.i.1.2", "L.ah0.2", "A.i.4.2", "N.i.2",
+    "P.ah0.1", "M.i.5.3", "L.ah0.3", "Q.ah0.0", "A.i.4.1", "B.i.2", "L.ah1.0", "T.wh1.2",
+    "T.wh2.3", "L.ah1.1", "A.i.1.2", "M.i.4.0", "L.ah1.2", "Q.ah0.1", "A.i.5.3", "M.i.4.3",
+    "L.ah1.3", "M.i.3.1", "P.wh2.3", "N.i.1", "P.wh1.2", "M.i.5.0", "A.i.4.0", "B.i.1",
+    "T.wh2.1", "A.i.4.3", "T.wh2.0", "A.i.3.1", "T.wh2.2", "M.i.5.1", "A.i.5.0", "M.i.6.0",
+    "P.wh2.1", "Q.wh1", "M.i.5.2", "P.wh2.0", "M.i.7.1", "N.i.4", "P.wh2.2", "A.i.5.1",
+    "T.wh3.2", "B.i.4", "A.i.6.0", "T.ah0.2", "T.wh3.3", "A.i.5.2", "M.i.3.2", "A.i.7.1",
+    "M.i.3.3", "Q.wh2", "M.i.7.2", "P.wh3.2", "T.wh3.1", "N.i.5", "P.ah0.2", "T.wh3.0",
+    "A.i.3.2", "B.i.5", "M.i.7.3", "Q.ah0.2", "A.i.3.3", "M.i.7.0", "P.wh3.3", "M.h.0.0",
+    "A.i.7.2", "N.i.3", "P.wh3.0", "A.i.7.3", "M.i.6.2", "P.wh3.1", "A.i.7.0", "T.ah1.2",
+    "B.i.3", "T.ah1.0", "A.h.0.0", "T.ah1.1", "M.h.1.2", "Q.wh3", "M.h.0.1", "A.i.6.2",
+    "M.h.0.2", "N.i.7", "P.ah1.1", "R.i.0", "A.h.1.2", "M.h.0.3", "B.i.7", "A.h.0.1",
+    "M.i.6.3", "A.h.0.2", "M.h.1.0", "A.h.0.3", "M.h.1.3", "P.ah1.2", "A.i.6.3", "M.h.1.1",
+    "P.ah1.0", "A.h.1.0", "M.i.6.1", "N.h.0", "A.h.1.3", "B.h.0", "K.0", "M.h.2.2",
+    "A.h.1.1", "T.ah0.3", "M.h.2.0", "A.i.6.1", "M.h.2.3", "P.ah0.3", "N.h.1", "N.i.6",
+    "M.h.2.1", "Q.ah1.0", "B.h.1", "K.1", "Q.ah0.3", "R.h.0", "A.h.2.2", "A.h.2.0",
+    "M.h.3.3", "A.h.2.3", "M.h.4.1", "B.i.6", "A.h.2.1", "R.h.1", "T.ah1.3", "M.h.3.0",
+    "C.0", "U.0", "U.1", "M.h.3.2", "N.h.2", "B.h.2", "K.2", "C.1",
+    "D.0.0", "R.h.2", "A.h.3.3", "A.h.4.1", "M.h.3.1", "U.2", "R.i.1", "A.h.3.0",
+    "M.h.4.3", "D.1.0", "Q.ah1.2", "S.0.0", "M.h.4.2", "A.h.3.2", "A.h.3.1", "M.h.4.0",
+    "A.h.4.3", "N.h.3", "A.h.4.2", "S.1.0", "B.h.3", "K.3", "A.h.4.0", "Q.ah1.1",
+    "C.2", "M.h.5.2", "M.h.5.0", "N.h.4", "R.h.3", "B.h.4", "M.h.5.1", "K.4",
+    "M.h.5.3", "P.ah1.3", "U.3", "A.h.5.2", "A.h.5.3", "D.2.0", "M.h.6.3", "R.h.4",
+    "A.h.5.0", "A.h.5.1", "U.4", "M.h.6.0", "C.3", "M.h.6.2", "N.h.5", "S.2.0",
+    "B.h.5", "M.h.6.1", "K.5", "Q.ah1.3", "A.h.6.3", "D.3.0", "R.h.5", "A.h.6.2",
+    "M.h.7.2", "A.h.6.0", "U.5", "A.h.6.1", "M.h.7.1", "C.4", "M.h.7.3", "N.h.6",
+    "S.3.0", "B.h.6", "K.6", "M.h.7.0", "A.h.7.3", "D.4.0", "R.h.6", "A.h.7.2",
+    "A.h.7.0", "U.6", "A.h.7.1", "C.5", "N.h.7", "S.4.0", "B.h.7", "C.6",
+    "D.5.0", "R.h.7", "K.7", "U.7", "C.7", "D.6.0", "S.5.0", "D.7.1",
+    "S.6.0", "D.7.0", "D.7.2", "S.7.0", "S.7.1", "D.7.3", "S.7.2", "S.7.3",
+)
+
+
+def emit(name, fn):
+    fn()
 
 
 def tile_layernormgrucell_pa_kernel(tc, x, h, W_irz, b_irz, W_hrz, b_hrz, out):
@@ -29,19 +93,18 @@ def tile_layernormgrucell_pa_kernel(tc, x, h, W_irz, b_irz, W_hrz, b_hrz, out):
     with ExitStack() as ctx:
         const = ctx.enter_context(tc.tile_pool(name="const", bufs=1))
         keep = ctx.enter_context(tc.tile_pool(name="keep", bufs=1))
-        rawp = ctx.enter_context(tc.tile_pool(name="rawp", bufs=5))
-        grp = ctx.enter_context(tc.tile_pool(name="grp", bufs=2))
-        vhp = ctx.enter_context(tc.tile_pool(name="vhp", bufs=3))
-        small = ctx.enter_context(tc.tile_pool(name="small", bufs=4))
-        ps_t = ctx.enter_context(tc.psum_pool(name="ps_t", bufs=4))
-        ps_a = ctx.enter_context(tc.psum_pool(name="ps_a", bufs=4))
+        rawp = ctx.enter_context(tc.tile_pool(name="rawp", bufs=RAW_BUFS))
+        grp = ctx.enter_context(tc.tile_pool(name="grp", bufs=GQ_BUFS))
+        gap = ctx.enter_context(tc.tile_pool(name="gap", bufs=GA_BUFS))
+        vp = ctx.enter_context(tc.tile_pool(name="vp", bufs=V_BUFS))
+        small = ctx.enter_context(tc.tile_pool(name="small", bufs=8))
+        ps_t = ctx.enter_context(tc.psum_pool(name="ps_t", bufs=PS_T))
+        ps_a = ctx.enter_context(tc.psum_pool(name="ps_a", bufs=PS_A))
 
         ident = const.tile([P, P], F32, name="ident")
         make_identity(nc, ident[:])
-        neghalf = const.tile([P, 1], F32, name="neghalf")
+        neghalf = const.tile([P, 4], F32, name="neghalf")
         nc.gpsimd.memset(neghalf[:], -0.5)
-        poshalf = const.tile([P, 1], F32, name="poshalf")
-        nc.gpsimd.memset(poshalf[:], 0.5)
         warm_in = const.tile([P, 1], F32, name="warm_in")
         nc.vector.memset(warm_in[:], 0.0)
         warm_out = const.tile([P, 1], F32, name="warm_out")
@@ -56,158 +119,245 @@ def tile_layernormgrucell_pa_kernel(tc, x, h, W_irz, b_irz, W_hrz, b_hrz, out):
             planes["w" + s] = keep.tile([P, N_BLOCKS, 2 * NB], U8, name="ws_%s" % s, align_bytes=64)
             codes["a" + s] = keep.tile([P, 2, 2 * NB], U32, name="ac_%s" % s, align_bytes=64)
             planes["a" + s] = keep.tile([P, 2, 2 * NB], U8, name="as_%s" % s, align_bytes=64)
-        v_i = [keep.tile([P, G], F32, name="v_i%d" % t) for t in range(N_TILES)]
-        junk = keep.tile([P, G], F32, name="junk")
+        junk = keep.tile([P, G], BF16, name="junk")
         part = {s: keep.tile([P, N_TILES, N_BLOCKS], F32, name="part_%s" % s) for s in ("i", "h")}
         ssd = {s: keep.tile([P, N_TILES], F32, name="ssd_%s" % s) for s in ("i", "h")}
         negmu = {s: keep.tile([P, N_TILES], F32, name="negmu_%s" % s) for s in ("i", "h")}
         r_i = keep.tile([P, N_TILES], F32, name="r_i")
-        q_i = keep.tile([P, N_TILES], F32, name="q_i")
+        w_g = keep.tile([P, N_TILES], F32, name="w_g")
+        w_e = keep.tile([P, N_TILES], F32, name="w_e")
+        nr_i = keep.tile([P, N_TILES], F32, name="nr_i")
+        nr_h = keep.tile([P, N_TILES], F32, name="nr_h")
+        ratio = keep.tile([P, N_TILES], F32, name="ratio")
+        cbias = keep.tile([P, N_TILES], F32, name="cbias")
+        dram = {"wi": W_irz, "wh": W_hrz, "ai": x, "ah": h}
+        live = {}
 
-        count = {"copies": 0}
+        def get(key, make):
+            if key not in live:
+                live[key] = make()
+            return live[key]
 
-        def load(src_rows, pieces):
-            raw = rawp.tile([P, 4, K], BF16, name="raw")
-            view = src_rows.rearrange("(j p) k -> p j k", p=P)
-            if pieces == 1:
-                nc.sync.dma_start(out=raw[:], in_=view)
-            else:
-                for j in range(4):
-                    nc.sync.dma_start(out=raw[:, j, :], in_=view[:, j, :])
-            return raw
+        def v_tile(s, t):
+            return get(("v", s, t), lambda: vp.tile([P, G], F32, name="v"))
 
-        def prep(raw, kind, code_ap, plane_ap):
-            gq = grp.tile([P, 8 * NB], BF16, name="gq", align_bytes=64)
-            words = gq[:].bitcast(F32)
-            if kind == "w":
-                dest = words.rearrange("q (g n u) -> q g n u", g=2, n=NB, u=2)
-            else:
-                dest = words.rearrange("q (j g r u) -> q j g r u", j=4, g=2, r=P, u=2)
-            for j in range(4):
+        def gq_tile(blk):
+            return get(("gq", blk), lambda: grp.tile([P, 8 * NB], BF16, name="gq", align_bytes=64))
+
+        def ga_tile(blk, j):
+            return get(("ga", blk, j), lambda: gap.tile([P, 2 * NB], BF16, name="ga", align_bytes=64))
+
+        def t_load(blk, j):
+            def go():
+                raw = rawp.tile([P, K], BF16, name="raw")
+                live[("raw", blk, j)] = raw
+                r0 = int(blk[2]) * NB + j * P
+                nc.sync.dma_start(out=raw[:], in_=dram[blk[:2]][r0:r0 + P, :])
+            return go
+
+        def t_bias(s, vec, gb):
+            cols = slice(gb * NB, (gb + 1) * NB)
+            return lambda: nc.sync.dma_start(out=bias[s][:, cols], in_=vec[cols].partition_broadcast(P))
+
+        def t_transpose(blk, j):
+            def go():
                 xt = ps_t.tile([P, 4, P], F32, name="xt")
-                rw = raw[:, j, :].bitcast(F32)
-                for s in range(4):
-                    nc.tensor.transpose(xt[:, s, :], rw[:, s * P:(s + 1) * P], ident[:])
-                src = xt[:].rearrange("q (g u) r -> q g r u", g=2, u=2)
-                if kind == "w":
-                    d = dest[:, :, j * P:(j + 1) * P, :]
+                live[("xt", blk, j)] = xt
+                rw = live[("raw", blk, j)][:].bitcast(F32)
+                for s4 in range(4):
+                    nc.tensor.transpose(xt[:, s4, :], rw[:, s4 * P:(s4 + 1) * P], ident[:])
+            return go
+
+        def t_copy(blk, j):
+            def go():
+                if blk[0] == "w":
+                    words = gq_tile(blk)[:].bitcast(F32)
+                    d = words.rearrange("q (g n u) -> q g n u", g=2, n=NB, u=2)[:, :, j * P:(j + 1) * P, :]
                 else:
-                    d = dest[:, j, :, :, :]
-                count["copies"] += 1
-                if count["copies"] % V_COPY_EVERY == 0:
+                    words = ga_tile(blk, j)[:].bitcast(F32)
+                    d = words.rearrange("q (g r u) -> q g r u", g=2, r=P, u=2)
+                src = live[("xt", blk, j)][:].rearrange("q (g u) r -> q g r u", g=2, u=2)
+                if (blk, j) in V_COPIES:
                     nc.vector.tensor_copy(out=d, in_=src)
                 else:
                     nc.scalar.copy(out=d, in_=src)
-            nc.vector.quantize_mx(out=code_ap.bitcast(FP8X4), scales=plane_ap, in_=gq[:])
+            return go
 
-        def mx_bias(s, t, gb, v):
-            acc = ps_a.tile([P, NB], F32, name="acc")
-            grp_i, j = divmod(t, 4)
-            for g in range(2):
-                a0 = (j * 2 + g) * P
-                nc.tensor.matmul_mx(
-                    out=acc[:],
-                    lhsT=codes["a" + s][:, grp_i, a0:a0 + P].bitcast(FP8X4),
-                    lhsT_scale=planes["a" + s][:, grp_i, a0:a0 + P],
-                    rhs=codes["w" + s][:, gb, g * NB:(g + 1) * NB].bitcast(FP8X4),
-                    rhs_scale=planes["w" + s][:, gb, g * NB:(g + 1) * NB],
-                    start=(g == 0),
-                    stop=(g == 1),
+        def t_quant(blk):
+            def go():
+                n = int(blk[2])
+                nc.vector.quantize_mx(
+                    out=codes[blk[:2]][:, n, :].bitcast(FP8X4), scales=planes[blk[:2]][:, n, :], in_=gq_tile(blk)[:],
                 )
-            cols = slice(gb * NB, (gb + 1) * NB)
-            nc.vector.scalar_tensor_tensor(
-                out=v[:, cols], in0=acc[:], scalar=1.0, in1=bias[s][:, cols],
-                op0=ALU.mult, op1=ALU.add, accum_out=part[s][:, t, gb:gb + 1],
-            )
+            return go
 
-        def stats(s, t, v):
-            t2 = small.tile([P, 2], F32, name="t2")
-            nc.gpsimd.tensor_tensor(out=t2[:], in0=part[s][:, t, 0:2], in1=part[s][:, t, 2:4], op=ALU.add)
-            nc.gpsimd.tensor_scalar(
-                out=negmu[s][:, t:t + 1], in0=t2[:, 0:1], scalar1=t2[:, 1:2], scalar2=-1.0 / G,
-                op0=ALU.add, op1=ALU.mult,
-            )
-            nc.scalar.activation(
-                out=junk[:], in_=v[:], func=ACT.Square, bias=negmu[s][:, t:t + 1], scale=1.0,
+        def t_quant_a(blk, j):
+            def go():
+                n = int(blk[2])
+                w = slice(j * 2 * P, (j + 1) * 2 * P)
+                nc.vector.quantize_mx(
+                    out=codes[blk[:2]][:, n, w].bitcast(FP8X4), scales=planes[blk[:2]][:, n, w], in_=ga_tile(blk, j)[:],
+                )
+            return go
+
+        def t_mx(s, t, gb):
+            def go():
+                acc = ps_a.tile([P, NB], F32, name="acc")
+                live[("acc", s, t, gb)] = acc
+                half, j = divmod(t, 4)
+                for g in range(2):
+                    a0 = (j * 2 + g) * P
+                    nc.tensor.matmul_mx(
+                        out=acc[:],
+                        lhsT=codes["a" + s][:, half, a0:a0 + P].bitcast(FP8X4),
+                        lhsT_scale=planes["a" + s][:, half, a0:a0 + P],
+                        rhs=codes["w" + s][:, gb, g * NB:(g + 1) * NB].bitcast(FP8X4),
+                        rhs_scale=planes["w" + s][:, gb, g * NB:(g + 1) * NB],
+                        start=(g == 0),
+                        stop=(g == 1),
+                    )
+            return go
+
+        def t_add(s, t, gb):
+            def go():
+                cols = slice(gb * NB, (gb + 1) * NB)
+                nc.vector.scalar_tensor_tensor(
+                    out=v_tile(s, t)[:, cols], in0=live[("acc", s, t, gb)][:], scalar=1.0, in1=bias[s][:, cols],
+                    op0=ALU.mult, op1=ALU.add, accum_out=part[s][:, t, gb:gb + 1],
+                )
+            return go
+
+        def t_negmean(s, t):
+            def go():
+                scr = small.tile([P, N_BLOCKS], F32, name="scr")
+                nc.scalar.activation(
+                    out=scr[:], in_=part[s][:, t, :], func=ACT.Identity, scale=-1.0 / G,
+                    accum_out=negmu[s][:, t:t + 1],
+                )
+            return go
+
+        def t_nrh(t):
+            c = slice(t, t + 1)
+            return lambda: nc.gpsimd.tensor_tensor(out=nr_h[:, c], in0=negmu["h"][:, c], in1=r_i[:, c], op=ALU.mult)
+
+        def t_square(s, t):
+            return lambda: nc.scalar.activation(
+                out=junk[:], in_=v_tile(s, t)[:], func=ACT.Square, bias=negmu[s][:, t:t + 1], scale=1.0,
                 accum_out=ssd[s][:, t:t + 1],
             )
-            ve = small.tile([P, 1], F32, name="ve")
-            nc.gpsimd.tensor_scalar(
-                out=ve[:], in0=ssd[s][:, t:t + 1], scalar1=1.0 / G, scalar2=EPS,
-                op0=ALU.mult, op1=ALU.add,
+
+        def t_rstd_i(half):
+            def go():
+                c = slice(4 * half, 4 * half + 4)
+                ve = small.tile([P, 4], F32, name="ve")
+                nc.gpsimd.tensor_scalar(
+                    out=ve[:], in0=ssd["i"][:, c], scalar1=1.0 / G, scalar2=EPS, op0=ALU.mult, op1=ALU.add,
+                )
+                nc.gpsimd.tensor_tensor(out=r_i[:, c], in0=ve[:], in1=neghalf[:], op=ALU.pow)
+                w = small.tile([P, 4], F32, name="w")
+                nc.gpsimd.tensor_tensor(out=w[:], in0=r_i[:, c], in1=r_i[:, c], op=ALU.mult)
+                nc.gpsimd.tensor_scalar(
+                    out=w_g[:, c], in0=w[:], scalar1=1.0 / G, scalar2=0.0, op0=ALU.mult, op1=ALU.add,
+                )
+                nc.gpsimd.tensor_scalar(
+                    out=w_e[:, c], in0=w[:], scalar1=EPS, scalar2=0.0, op0=ALU.mult, op1=ALU.add,
+                )
+                nc.gpsimd.tensor_tensor(out=nr_i[:, c], in0=negmu["i"][:, c], in1=r_i[:, c], op=ALU.mult)
+            return go
+
+        def t_rstd_h(t):
+            def go():
+                c = slice(t, t + 1)
+                xr = small.tile([P, 1], F32, name="xr")
+                nc.gpsimd.tensor_scalar(
+                    out=xr[:], in0=ssd["h"][:, c], scalar1=w_g[:, c], scalar2=w_e[:, c], op0=ALU.mult, op1=ALU.add,
+                )
+                nc.gpsimd.tensor_tensor(out=ratio[:, c], in0=xr[:], in1=neghalf[:, 0:1], op=ALU.pow)
+            return go
+
+        def t_shift(t):
+            def go():
+                c = slice(t, t + 1)
+                nc.gpsimd.tensor_scalar(
+                    out=cbias[:, c], in0=ratio[:, c], scalar1=nr_h[:, c], scalar2=nr_i[:, c], op0=ALU.mult, op1=ALU.add,
+                )
+            return go
+
+        def t_combine(t):
+            def go():
+                vh = v_tile("h", t)
+                if t in G_COMBINES:
+                    nc.gpsimd.tensor_scalar(
+                        out=vh[:], in0=vh[:], scalar1=ratio[:, t:t + 1], scalar2=0.0, op0=ALU.mult, op1=ALU.add,
+                    )
+                    nc.gpsimd.tensor_tensor(out=vh[:], in0=vh[:], in1=v_tile("i", t)[:], op=ALU.add)
+                else:
+                    nc.vector.scalar_tensor_tensor(
+                        out=vh[:], in0=vh[:], scalar=ratio[:, t:t + 1], in1=v_tile("i", t)[:],
+                        op0=ALU.mult, op1=ALU.add,
+                    )
+            return go
+
+        def piece(t, q):
+            w = G // D_SPLIT.get(t, 1)
+            return slice(q * w, (q + 1) * w)
+
+        def t_sigmoid(t, q):
+            return lambda: nc.scalar.activation(
+                out=v_tile("h", t)[:, piece(t, q)], in_=v_tile("h", t)[:, piece(t, q)], func=ACT.Sigmoid,
+                bias=cbias[:, t:t + 1], scale=r_i[:, t:t + 1],
             )
-            return ve
 
-        raws = {}
-        raws["wi0"] = load(W_irz[0:NB, :], 4)
-        raws["ai0"] = load(x[0:NB, :], 1)
-        nc.sync.dma_start(out=bias["i"][:], in_=b_irz.partition_broadcast(P))
-
-        def prep_w(s, gb):
-            prep(raws["w%s%d" % (s, gb)], "w", codes["w" + s][:, gb, :], planes["w" + s][:, gb, :])
-
-        def prep_a(s, g2):
-            prep(raws["a%s%d" % (s, g2)], "a", codes["a" + s][:, g2, :], planes["a" + s][:, g2, :])
-
-        prep_w("i", 0)
-        raws["wi1"] = load(W_irz[NB:2 * NB, :], 1)
-        prep_a("i", 0)
-        raws["ai1"] = load(x[NB:2 * NB, :], 1)
-        for t in range(4):
-            mx_bias("i", t, 0, v_i[t])
-        prep_w("i", 1)
-        raws["wi2"] = load(W_irz[2 * NB:3 * NB, :], 1)
-        for t in range(4):
-            mx_bias("i", t, 1, v_i[t])
-        prep_a("i", 1)
-        raws["wi3"] = load(W_irz[3 * NB:4 * NB, :], 1)
-        for gb in range(2):
-            for t in range(4, 8):
-                mx_bias("i", t, gb, v_i[t])
-        prep_w("i", 2)
-        raws["ah0"] = load(h[0:NB, :], 1)
-        for t in range(N_TILES):
-            mx_bias("i", t, 2, v_i[t])
-        prep_w("i", 3)
-        raws["wh0"] = load(W_hrz[0:NB, :], 1)
-        nc.sync.dma_start(out=bias["h"][:], in_=b_hrz.partition_broadcast(P))
-        for t in range(N_TILES):
-            mx_bias("i", t, 3, v_i[t])
-            ve = stats("i", t, v_i[t])
-            nc.gpsimd.tensor_tensor(out=r_i[:, t:t + 1], in0=ve[:], in1=neghalf[:], op=ALU.pow)
-            nc.gpsimd.tensor_tensor(out=q_i[:, t:t + 1], in0=ve[:], in1=poshalf[:], op=ALU.pow)
-
-        prep_a("h", 0)
-        raws["ah1"] = load(h[NB:2 * NB, :], 1)
-        prep_w("h", 0)
-        raws["wh1"] = load(W_hrz[NB:2 * NB, :], 1)
-        prep_a("h", 1)
-        raws["wh2"] = load(W_hrz[2 * NB:3 * NB, :], 1)
-        prep_w("h", 1)
-        raws["wh3"] = load(W_hrz[3 * NB:4 * NB, :], 1)
-        prep_w("h", 2)
-        prep_w("h", 3)
-
-        for t in range(N_TILES):
-            v_h = vhp.tile([P, G], F32, name="v_h")
-            for gb in range(N_BLOCKS):
-                mx_bias("h", t, gb, v_h)
-            ve = stats("h", t, v_h)
-            r_h = small.tile([P, 1], F32, name="r_h")
-            nc.gpsimd.tensor_tensor(out=r_h[:], in0=ve[:], in1=neghalf[:], op=ALU.pow)
-            ratio = small.tile([P, 1], F32, name="ratio")
-            nc.gpsimd.tensor_tensor(out=ratio[:], in0=r_h[:], in1=q_i[:, t:t + 1], op=ALU.mult)
-            nc.vector.scalar_tensor_tensor(
-                out=v_h[:], in0=v_h[:], scalar=ratio[:], in1=v_i[t][:], op0=ALU.mult, op1=ALU.add,
+        def t_store(t, q):
+            return lambda: nc.sync.dma_start(
+                out=out[t * P:(t + 1) * P, piece(t, q)], in_=v_tile("h", t)[:, piece(t, q)],
             )
-            shift = small.tile([P, 1], F32, name="shift")
-            nc.gpsimd.tensor_scalar(
-                out=shift[:], in0=negmu["h"][:, t:t + 1], scalar1=ratio[:], scalar2=negmu["i"][:, t:t + 1],
-                op0=ALU.mult, op1=ALU.add,
-            )
-            cbias = small.tile([P, 1], F32, name="cbias")
-            nc.gpsimd.tensor_tensor(out=cbias[:], in0=shift[:], in1=r_i[:, t:t + 1], op=ALU.mult)
-            nc.scalar.activation(
-                out=v_h[:], in_=v_h[:], func=ACT.Sigmoid, bias=cbias[:], scale=r_i[:, t:t + 1],
-            )
-            nc.sync.dma_start(out=out[t * P:(t + 1) * P, :], in_=v_h[:])
+
+        tasks = {}
+        natural = []
+
+        def add(name, fn):
+            tasks[name] = fn
+            natural.append(name)
+
+        chunks = []
+        for item in LOAD_ORDER:
+            if item[0] == "b":
+                add("L.%s" % item, t_bias(item[1], b_irz if item[1] == "i" else b_hrz, int(item[2])))
+            else:
+                js = [int(item[4])] if len(item) > 3 else [0, 1, 2, 3]
+                for j in js:
+                    chunks.append((item[:3], j))
+                    add("L.%s.%d" % (item[:3], j), t_load(item[:3], j))
+        for blk, j in chunks:
+            add("T.%s.%d" % (blk, j), t_transpose(blk, j))
+            add("P.%s.%d" % (blk, j), t_copy(blk, j))
+            if blk[0] == "a":
+                add("Q.%s.%d" % (blk, j), t_quant_a(blk, j))
+            elif j == 3:
+                add("Q.%s" % blk, t_quant(blk))
+        for s in ("i", "h"):
+            for t in range(N_TILES):
+                for gb in range(N_BLOCKS):
+                    add("M.%s.%d.%d" % (s, t, gb), t_mx(s, t, gb))
+                    add("A.%s.%d.%d" % (s, t, gb), t_add(s, t, gb))
+                add("N.%s.%d" % (s, t), t_negmean(s, t))
+                if s == "h":
+                    add("K.%d" % t, t_nrh(t))
+                add("B.%s.%d" % (s, t), t_square(s, t))
+                if s == "i":
+                    if t % 4 == 3:
+                        add("R.i.%d" % (t // 4), t_rstd_i(t // 4))
+                else:
+                    add("R.h.%d" % t, t_rstd_h(t))
+                    add("U.%d" % t, t_shift(t))
+                    add("C.%d" % t, t_combine(t))
+                    for q in range(D_SPLIT.get(t, 1)):
+                        add("D.%d.%d" % (t, q), t_sigmoid(t, q))
+                        add("S.%d.%d" % (t, q), t_store(t, q))
+
+        order = ORDER if ORDER else natural
+        assert sorted(order) == sorted(natural)
+        with tc.manual_schedule():
+            for name in order:
+                emit(name, tasks[name])

@@ -16,348 +16,268 @@ B = 1024
 K = 1024
 G = 2048
 EPS = 1e-5
-NB = 512
+BANK = 512
+PASSES = K // 512
 N_TILES = B // P
-N_BLOCKS = G // NB
+N_BLOCKS = G // BANK
+WORDS = PASSES * P
 FLOPS = 2 * 2 * B * K * G
 
-RAW_BUFS = 16
-GQ_BUFS = 3
-GA_BUFS = 6
-V_BUFS = 11
-PS_T = 4
-PS_A = 4
-LOAD_ORDER = ("wi0", "ai0.0", "ai0.1", "bi0", "wi1", "bi1", "wi2", "bi2", "wi3", "bi3", "ai0.2", "ai0.3", "ai1.0", "ai1.1", "ai1.2", "ai1.3", "wh0", "ah0.0", "ah0.1", "bh0", "wh1", "bh1", "wh2", "bh2", "wh3", "bh3", "ah0.2", "ah0.3", "ah1.0", "ah1.1", "ah1.2", "ah1.3")
-V_COPIES = frozenset((("ah0", 3), ("wh0", 3), ("ah1", 3), ("wh1", 3), ("wh2", 3), ("wh3", 3)))
-G_COMBINES = frozenset(())
-D_SPLIT = {7: 4}
-ORDER = (
-    "L.wi0.0", "L.wi0.1", "L.wi0.2", "L.wi0.3", "L.ai0.0", "L.ai0.1", "L.bi0", "L.wi1.0",
-    "L.wi1.1", "T.wi0.0", "L.wi1.2", "T.wi0.1", "L.wi1.3", "T.wi0.2", "P.wi0.1", "L.bi1",
-    "P.wi0.0", "T.wi0.3", "P.wi0.2", "L.wi2.0", "P.wi0.3", "L.wi2.1", "T.ai0.1", "L.wi2.2",
-    "T.ai0.0", "Q.wi0", "P.ai0.1", "L.wi2.3", "T.wi1.0", "P.ai0.0", "L.bi2", "T.wi1.1",
-    "P.wi1.0", "Q.ai0.0", "L.wi3.0", "Q.ai0.1", "T.wi1.2", "P.wi1.1", "L.wi3.1", "T.wi1.3",
-    "P.wi1.2", "L.wi3.2", "M.i.1.0", "P.wi1.3", "L.wi3.3", "M.i.0.0", "Q.wi1", "L.bi3",
-    "T.wi2.0", "T.wi2.1", "L.ai0.2", "P.wi2.0", "T.wi2.2", "A.i.0.0", "L.ai0.3", "T.wi2.3",
-    "P.wi2.2", "A.i.1.0", "L.ai1.0", "M.i.0.1", "P.wi2.3", "L.ai1.1", "M.i.1.1", "P.wi2.1",
-    "L.ai1.2", "T.wi3.0", "Q.wi2", "T.wi3.1", "L.ai1.3", "P.wi3.0", "T.wi3.2", "L.wh0.0",
-    "T.wi3.3", "P.wi3.1", "A.i.1.1", "L.wh0.1", "P.wi3.2", "M.i.0.2", "A.i.0.1", "L.wh0.2",
-    "P.wi3.3", "T.ai0.2", "L.wh0.3", "T.ai0.3", "Q.wi3", "P.ai0.2", "L.ah0.0", "T.ai1.0",
-    "P.ai0.3", "L.ah0.1", "T.ai1.1", "Q.ai0.2", "P.ai1.0", "A.i.0.2", "L.bh0", "T.ai1.2",
-    "M.i.0.3", "Q.ai0.3", "L.wh1.0", "P.ai1.2", "Q.ai1.0", "M.i.1.3", "L.wh1.1", "P.ai1.1",
-    "A.i.0.3", "M.i.2.1", "L.wh1.2", "A.i.1.3", "M.i.2.0", "L.wh1.3", "Q.ai1.1", "T.wh0.0",
-    "A.i.2.1", "L.bh1", "T.wh0.3", "P.wh0.0", "T.ai1.3", "L.wh2.0", "P.wh0.3", "T.wh0.1",
-    "N.i.0", "P.ai1.3", "T.wh0.2", "L.wh2.1", "A.i.2.0", "T.ah0.0", "L.wh2.2", "P.wh0.1",
-    "M.i.2.2", "Q.ai1.2", "P.wh0.2", "L.wh2.3", "Q.ai1.3", "M.i.3.0", "P.ah0.0", "A.i.2.2",
-    "L.bh2", "M.i.2.3", "B.i.0", "A.i.3.0", "L.wh3.0", "T.ah0.1", "A.i.2.3", "T.wh1.0",
-    "L.wh3.1", "T.wh1.3", "L.wh3.2", "Q.wh0", "T.wh1.1", "M.i.4.2", "L.wh3.3", "P.wh1.0",
-    "L.bh3", "M.i.4.1", "P.wh1.3", "P.wh1.1", "M.i.1.2", "L.ah0.2", "A.i.4.2", "N.i.2",
-    "P.ah0.1", "M.i.5.3", "L.ah0.3", "Q.ah0.0", "A.i.4.1", "B.i.2", "L.ah1.0", "T.wh1.2",
-    "T.wh2.3", "L.ah1.1", "A.i.1.2", "M.i.4.0", "L.ah1.2", "Q.ah0.1", "A.i.5.3", "M.i.4.3",
-    "L.ah1.3", "M.i.3.1", "P.wh2.3", "N.i.1", "P.wh1.2", "M.i.5.0", "A.i.4.0", "B.i.1",
-    "T.wh2.1", "A.i.4.3", "T.wh2.0", "A.i.3.1", "T.wh2.2", "M.i.5.1", "A.i.5.0", "M.i.6.0",
-    "P.wh2.1", "Q.wh1", "M.i.5.2", "P.wh2.0", "M.i.7.1", "N.i.4", "P.wh2.2", "A.i.5.1",
-    "T.wh3.2", "B.i.4", "A.i.6.0", "T.ah0.2", "T.wh3.3", "A.i.5.2", "M.i.3.2", "A.i.7.1",
-    "M.i.3.3", "Q.wh2", "M.i.7.2", "P.wh3.2", "T.wh3.1", "N.i.5", "P.ah0.2", "T.wh3.0",
-    "A.i.3.2", "B.i.5", "M.i.7.3", "Q.ah0.2", "A.i.3.3", "M.i.7.0", "P.wh3.3", "M.h.0.0",
-    "A.i.7.2", "N.i.3", "P.wh3.0", "A.i.7.3", "M.i.6.2", "P.wh3.1", "A.i.7.0", "T.ah1.2",
-    "B.i.3", "T.ah1.0", "A.h.0.0", "T.ah1.1", "M.h.1.2", "Q.wh3", "M.h.0.1", "A.i.6.2",
-    "M.h.0.2", "N.i.7", "P.ah1.1", "R.i.0", "A.h.1.2", "M.h.0.3", "B.i.7", "A.h.0.1",
-    "M.i.6.3", "A.h.0.2", "M.h.1.0", "A.h.0.3", "M.h.1.3", "P.ah1.2", "A.i.6.3", "M.h.1.1",
-    "P.ah1.0", "A.h.1.0", "M.i.6.1", "N.h.0", "A.h.1.3", "B.h.0", "K.0", "M.h.2.2",
-    "A.h.1.1", "T.ah0.3", "M.h.2.0", "A.i.6.1", "M.h.2.3", "P.ah0.3", "N.h.1", "N.i.6",
-    "M.h.2.1", "Q.ah1.0", "B.h.1", "K.1", "Q.ah0.3", "R.h.0", "A.h.2.2", "A.h.2.0",
-    "M.h.3.3", "A.h.2.3", "M.h.4.1", "B.i.6", "A.h.2.1", "R.h.1", "T.ah1.3", "M.h.3.0",
-    "C.0", "U.0", "U.1", "M.h.3.2", "N.h.2", "B.h.2", "K.2", "C.1",
-    "D.0.0", "R.h.2", "A.h.3.3", "A.h.4.1", "M.h.3.1", "U.2", "R.i.1", "A.h.3.0",
-    "M.h.4.3", "D.1.0", "Q.ah1.2", "S.0.0", "M.h.4.2", "A.h.3.2", "A.h.3.1", "M.h.4.0",
-    "A.h.4.3", "N.h.3", "A.h.4.2", "S.1.0", "B.h.3", "K.3", "A.h.4.0", "Q.ah1.1",
-    "C.2", "M.h.5.2", "M.h.5.0", "N.h.4", "R.h.3", "B.h.4", "M.h.5.1", "K.4",
-    "M.h.5.3", "P.ah1.3", "U.3", "A.h.5.2", "A.h.5.3", "D.2.0", "M.h.6.3", "R.h.4",
-    "A.h.5.0", "A.h.5.1", "U.4", "M.h.6.0", "C.3", "M.h.6.2", "N.h.5", "S.2.0",
-    "B.h.5", "M.h.6.1", "K.5", "Q.ah1.3", "A.h.6.3", "D.3.0", "R.h.5", "A.h.6.2",
-    "M.h.7.2", "A.h.6.0", "U.5", "A.h.6.1", "M.h.7.1", "C.4", "M.h.7.3", "N.h.6",
-    "S.3.0", "B.h.6", "K.6", "M.h.7.0", "A.h.7.3", "D.4.0", "R.h.6", "A.h.7.2",
-    "A.h.7.0", "U.6", "A.h.7.1", "C.5", "N.h.7", "S.4.0", "B.h.7", "C.6",
-    "D.5.0", "R.h.7", "K.7", "U.7", "C.7", "D.6.0", "S.5.0", "D.7.1",
-    "S.6.0", "D.7.0", "D.7.2", "S.7.0", "S.7.1", "D.7.3", "S.7.2", "S.7.3",
-)
-
-
-def emit(name, fn):
-    fn()
+SIDES = ("x", "h")
+JOBS = tuple((side, t) for side in SIDES for t in range(N_TILES))
+N_JOBS = len(JOBS)
+EARLY = 2
+HALVES = 2
 
 
 def tile_layernormgrucell_pa_kernel(tc, x, h, W_irz, b_irz, W_hrz, b_hrz, out):
     nc = tc.nc
+    act_dram = {"x": x, "h": h}
+    wgt_dram = {"x": W_irz, "h": W_hrz}
+    bias_dram = {"x": b_irz, "h": b_hrz}
+
     with ExitStack() as ctx:
         const = ctx.enter_context(tc.tile_pool(name="const", bufs=1))
         keep = ctx.enter_context(tc.tile_pool(name="keep", bufs=1))
-        rawp = ctx.enter_context(tc.tile_pool(name="rawp", bufs=RAW_BUFS))
-        grp = ctx.enter_context(tc.tile_pool(name="grp", bufs=GQ_BUFS))
-        gap = ctx.enter_context(tc.tile_pool(name="gap", bufs=GA_BUFS))
-        vp = ctx.enter_context(tc.tile_pool(name="vp", bufs=V_BUFS))
-        small = ctx.enter_context(tc.tile_pool(name="small", bufs=8))
-        ps_t = ctx.enter_context(tc.psum_pool(name="ps_t", bufs=PS_T))
-        ps_a = ctx.enter_context(tc.psum_pool(name="ps_a", bufs=PS_A))
+        raw_pool = ctx.enter_context(tc.tile_pool(name="raw_pool", bufs=16))
+        wq_pool = ctx.enter_context(tc.tile_pool(name="wq_pool", bufs=3))
+        aq_pool = ctx.enter_context(tc.tile_pool(name="aq_pool", bufs=6))
+        v_pool = ctx.enter_context(tc.tile_pool(name="v_pool", bufs=N_TILES + 3))
+        tiny = ctx.enter_context(tc.tile_pool(name="tiny", bufs=4))
+        tr_psum = ctx.enter_context(tc.psum_pool(name="tr_psum", bufs=5))
+        acc_psum = ctx.enter_context(tc.psum_pool(name="acc_psum", bufs=3))
 
         ident = const.tile([P, P], F32, name="ident")
         make_identity(nc, ident[:])
-        neghalf = const.tile([P, 4], F32, name="neghalf")
-        nc.gpsimd.memset(neghalf[:], -0.5)
+        neg_half = const.tile([P, 1], F32, name="neg_half")
+        nc.gpsimd.memset(neg_half[:], -0.5)
+        pos_half = const.tile([P, 1], F32, name="pos_half")
+        nc.gpsimd.memset(pos_half[:], 0.5)
         warm_in = const.tile([P, 1], F32, name="warm_in")
         nc.vector.memset(warm_in[:], 0.0)
         warm_out = const.tile([P, 1], F32, name="warm_out")
         nc.scalar.activation(out=warm_out[:], in_=warm_in[:], func=ACT.Sigmoid)
 
-        bias = {}
-        codes = {}
-        planes = {}
-        for s in ("i", "h"):
-            bias[s] = const.tile([P, G], BF16, name="bias_%s" % s)
-            codes["w" + s] = keep.tile([P, N_BLOCKS, 2 * NB], U32, name="wc_%s" % s, align_bytes=64)
-            planes["w" + s] = keep.tile([P, N_BLOCKS, 2 * NB], U8, name="ws_%s" % s, align_bytes=64)
-            codes["a" + s] = keep.tile([P, 2, 2 * NB], U32, name="ac_%s" % s, align_bytes=64)
-            planes["a" + s] = keep.tile([P, 2, 2 * NB], U8, name="as_%s" % s, align_bytes=64)
-        junk = keep.tile([P, G], BF16, name="junk")
-        part = {s: keep.tile([P, N_TILES, N_BLOCKS], F32, name="part_%s" % s) for s in ("i", "h")}
-        ssd = {s: keep.tile([P, N_TILES], F32, name="ssd_%s" % s) for s in ("i", "h")}
-        negmu = {s: keep.tile([P, N_TILES], F32, name="negmu_%s" % s) for s in ("i", "h")}
-        r_i = keep.tile([P, N_TILES], F32, name="r_i")
-        w_g = keep.tile([P, N_TILES], F32, name="w_g")
-        w_e = keep.tile([P, N_TILES], F32, name="w_e")
-        nr_i = keep.tile([P, N_TILES], F32, name="nr_i")
-        nr_h = keep.tile([P, N_TILES], F32, name="nr_h")
+        bias_bc = {}
+        w_codes, w_scales, a_codes, a_scales = {}, {}, {}, {}
+        bank_sum, neg_mean, sq_dev = {}, {}, {}
+        for s in SIDES:
+            bias_bc[s] = const.tile([P, G], BF16, name="bias_bc_%s" % s)
+            w_codes[s] = keep.tile([P, N_BLOCKS, PASSES * BANK], U32, name="w_codes_%s" % s, align_bytes=64)
+            w_scales[s] = keep.tile([P, N_BLOCKS, PASSES * BANK], U8, name="w_scales_%s" % s, align_bytes=64)
+            a_codes[s] = keep.tile([P, N_TILES, WORDS], U32, name="a_codes_%s" % s, align_bytes=64)
+            a_scales[s] = keep.tile([P, N_TILES, WORDS], U8, name="a_scales_%s" % s, align_bytes=64)
+            bank_sum[s] = keep.tile([P, N_TILES, N_BLOCKS], F32, name="bank_sum_%s" % s)
+            neg_mean[s] = keep.tile([P, N_TILES], F32, name="neg_mean_%s" % s)
+            sq_dev[s] = keep.tile([P, N_TILES], F32, name="sq_dev_%s" % s)
+        squares_out = keep.tile([P, G], BF16, name="squares_out")
+        r_x = keep.tile([P, N_TILES], F32, name="r_x")
+        s_x = keep.tile([P, N_TILES], F32, name="s_x")
+        nr_x = keep.tile([P, N_TILES], F32, name="nr_x")
         ratio = keep.tile([P, N_TILES], F32, name="ratio")
-        cbias = keep.tile([P, N_TILES], F32, name="cbias")
-        dram = {"wi": W_irz, "wh": W_hrz, "ai": x, "ah": h}
-        live = {}
+        shift = keep.tile([P, N_TILES], F32, name="shift")
 
-        def get(key, make):
-            if key not in live:
-                live[key] = make()
-            return live[key]
+        raw = {}
+        turned = {}
+        grouped = {}
+        acc = {}
+        v = {}
 
-        def v_tile(s, t):
-            return get(("v", s, t), lambda: vp.tile([P, G], F32, name="v"))
+        def load(key, rows):
+            raw[key] = raw_pool.tile([P, K], BF16, name="raw")
+            nc.sync.dma_start(out=raw[key][:], in_=rows)
 
-        def gq_tile(blk):
-            return get(("gq", blk), lambda: grp.tile([P, 8 * NB], BF16, name="gq", align_bytes=64))
+        def transpose(key):
+            turned[key] = tr_psum.tile([P, 2 * PASSES, P], F32, name="turned")
+            words = raw[key][:].bitcast(F32)
+            for blk in range(2 * PASSES):
+                nc.tensor.transpose(turned[key][:, blk, :], words[:, blk * P:(blk + 1) * P], ident[:])
 
-        def ga_tile(blk, j):
-            return get(("ga", blk, j), lambda: gap.tile([P, 2 * NB], BF16, name="ga", align_bytes=64))
-
-        def t_load(blk, j):
-            def go():
-                raw = rawp.tile([P, K], BF16, name="raw")
-                live[("raw", blk, j)] = raw
-                r0 = int(blk[2]) * NB + j * P
-                nc.sync.dma_start(out=raw[:], in_=dram[blk[:2]][r0:r0 + P, :])
-            return go
-
-        def t_bias(s, vec, gb):
-            cols = slice(gb * NB, (gb + 1) * NB)
-            return lambda: nc.sync.dma_start(out=bias[s][:, cols], in_=vec[cols].partition_broadcast(P))
-
-        def t_transpose(blk, j):
-            def go():
-                xt = ps_t.tile([P, 4, P], F32, name="xt")
-                live[("xt", blk, j)] = xt
-                rw = live[("raw", blk, j)][:].bitcast(F32)
-                for s4 in range(4):
-                    nc.tensor.transpose(xt[:, s4, :], rw[:, s4 * P:(s4 + 1) * P], ident[:])
-            return go
-
-        def t_copy(blk, j):
-            def go():
-                if blk[0] == "w":
-                    words = gq_tile(blk)[:].bitcast(F32)
-                    d = words.rearrange("q (g n u) -> q g n u", g=2, n=NB, u=2)[:, :, j * P:(j + 1) * P, :]
-                else:
-                    words = ga_tile(blk, j)[:].bitcast(F32)
-                    d = words.rearrange("q (g r u) -> q g r u", g=2, r=P, u=2)
-                src = live[("xt", blk, j)][:].rearrange("q (g u) r -> q g r u", g=2, u=2)
-                if (blk, j) in V_COPIES:
-                    nc.vector.tensor_copy(out=d, in_=src)
-                else:
-                    nc.scalar.copy(out=d, in_=src)
-            return go
-
-        def t_quant(blk):
-            def go():
-                n = int(blk[2])
-                nc.vector.quantize_mx(
-                    out=codes[blk[:2]][:, n, :].bitcast(FP8X4), scales=planes[blk[:2]][:, n, :], in_=gq_tile(blk)[:],
-                )
-            return go
-
-        def t_quant_a(blk, j):
-            def go():
-                n = int(blk[2])
-                w = slice(j * 2 * P, (j + 1) * 2 * P)
-                nc.vector.quantize_mx(
-                    out=codes[blk[:2]][:, n, w].bitcast(FP8X4), scales=planes[blk[:2]][:, n, w], in_=ga_tile(blk, j)[:],
-                )
-            return go
-
-        def t_mx(s, t, gb):
-            def go():
-                acc = ps_a.tile([P, NB], F32, name="acc")
-                live[("acc", s, t, gb)] = acc
-                half, j = divmod(t, 4)
-                for g in range(2):
-                    a0 = (j * 2 + g) * P
-                    nc.tensor.matmul_mx(
-                        out=acc[:],
-                        lhsT=codes["a" + s][:, half, a0:a0 + P].bitcast(FP8X4),
-                        lhsT_scale=planes["a" + s][:, half, a0:a0 + P],
-                        rhs=codes["w" + s][:, gb, g * NB:(g + 1) * NB].bitcast(FP8X4),
-                        rhs_scale=planes["w" + s][:, gb, g * NB:(g + 1) * NB],
-                        start=(g == 0),
-                        stop=(g == 1),
-                    )
-            return go
-
-        def t_add(s, t, gb):
-            def go():
-                cols = slice(gb * NB, (gb + 1) * NB)
-                nc.vector.scalar_tensor_tensor(
-                    out=v_tile(s, t)[:, cols], in0=live[("acc", s, t, gb)][:], scalar=1.0, in1=bias[s][:, cols],
-                    op0=ALU.mult, op1=ALU.add, accum_out=part[s][:, t, gb:gb + 1],
-                )
-            return go
-
-        def t_negmean(s, t):
-            def go():
-                scr = small.tile([P, N_BLOCKS], F32, name="scr")
-                nc.scalar.activation(
-                    out=scr[:], in_=part[s][:, t, :], func=ACT.Identity, scale=-1.0 / G,
-                    accum_out=negmu[s][:, t:t + 1],
-                )
-            return go
-
-        def t_nrh(t):
-            c = slice(t, t + 1)
-            return lambda: nc.gpsimd.tensor_tensor(out=nr_h[:, c], in0=negmu["h"][:, c], in1=r_i[:, c], op=ALU.mult)
-
-        def t_square(s, t):
-            return lambda: nc.scalar.activation(
-                out=junk[:], in_=v_tile(s, t)[:], func=ACT.Square, bias=negmu[s][:, t:t + 1], scale=1.0,
-                accum_out=ssd[s][:, t:t + 1],
-            )
-
-        def t_rstd_i(half):
-            def go():
-                c = slice(4 * half, 4 * half + 4)
-                ve = small.tile([P, 4], F32, name="ve")
-                nc.gpsimd.tensor_scalar(
-                    out=ve[:], in0=ssd["i"][:, c], scalar1=1.0 / G, scalar2=EPS, op0=ALU.mult, op1=ALU.add,
-                )
-                nc.gpsimd.tensor_tensor(out=r_i[:, c], in0=ve[:], in1=neghalf[:], op=ALU.pow)
-                w = small.tile([P, 4], F32, name="w")
-                nc.gpsimd.tensor_tensor(out=w[:], in0=r_i[:, c], in1=r_i[:, c], op=ALU.mult)
-                nc.gpsimd.tensor_scalar(
-                    out=w_g[:, c], in0=w[:], scalar1=1.0 / G, scalar2=0.0, op0=ALU.mult, op1=ALU.add,
-                )
-                nc.gpsimd.tensor_scalar(
-                    out=w_e[:, c], in0=w[:], scalar1=EPS, scalar2=0.0, op0=ALU.mult, op1=ALU.add,
-                )
-                nc.gpsimd.tensor_tensor(out=nr_i[:, c], in0=negmu["i"][:, c], in1=r_i[:, c], op=ALU.mult)
-            return go
-
-        def t_rstd_h(t):
-            def go():
-                c = slice(t, t + 1)
-                xr = small.tile([P, 1], F32, name="xr")
-                nc.gpsimd.tensor_scalar(
-                    out=xr[:], in0=ssd["h"][:, c], scalar1=w_g[:, c], scalar2=w_e[:, c], op0=ALU.mult, op1=ALU.add,
-                )
-                nc.gpsimd.tensor_tensor(out=ratio[:, c], in0=xr[:], in1=neghalf[:, 0:1], op=ALU.pow)
-            return go
-
-        def t_shift(t):
-            def go():
-                c = slice(t, t + 1)
-                nc.gpsimd.tensor_scalar(
-                    out=cbias[:, c], in0=ratio[:, c], scalar1=nr_h[:, c], scalar2=nr_i[:, c], op0=ALU.mult, op1=ALU.add,
-                )
-            return go
-
-        def t_combine(t):
-            def go():
-                vh = v_tile("h", t)
-                if t in G_COMBINES:
-                    nc.gpsimd.tensor_scalar(
-                        out=vh[:], in0=vh[:], scalar1=ratio[:, t:t + 1], scalar2=0.0, op0=ALU.mult, op1=ALU.add,
-                    )
-                    nc.gpsimd.tensor_tensor(out=vh[:], in0=vh[:], in1=v_tile("i", t)[:], op=ALU.add)
-                else:
-                    nc.vector.scalar_tensor_tensor(
-                        out=vh[:], in0=vh[:], scalar=ratio[:, t:t + 1], in1=v_tile("i", t)[:],
-                        op0=ALU.mult, op1=ALU.add,
-                    )
-            return go
-
-        def piece(t, q):
-            w = G // D_SPLIT.get(t, 1)
-            return slice(q * w, (q + 1) * w)
-
-        def t_sigmoid(t, q):
-            return lambda: nc.scalar.activation(
-                out=v_tile("h", t)[:, piece(t, q)], in_=v_tile("h", t)[:, piece(t, q)], func=ACT.Sigmoid,
-                bias=cbias[:, t:t + 1], scale=r_i[:, t:t + 1],
-            )
-
-        def t_store(t, q):
-            return lambda: nc.sync.dma_start(
-                out=out[t * P:(t + 1) * P, piece(t, q)], in_=v_tile("h", t)[:, piece(t, q)],
-            )
-
-        tasks = {}
-        natural = []
-
-        def add(name, fn):
-            tasks[name] = fn
-            natural.append(name)
-
-        chunks = []
-        for item in LOAD_ORDER:
-            if item[0] == "b":
-                add("L.%s" % item, t_bias(item[1], b_irz if item[1] == "i" else b_hrz, int(item[2])))
+        def regroup(key, dest, on_vector):
+            src = turned[key][:].rearrange("q (g u) r -> q g r u", g=PASSES, u=2)
+            if on_vector:
+                nc.vector.tensor_copy(out=dest, in_=src)
             else:
-                js = [int(item[4])] if len(item) > 3 else [0, 1, 2, 3]
-                for j in js:
-                    chunks.append((item[:3], j))
-                    add("L.%s.%d" % (item[:3], j), t_load(item[:3], j))
-        for blk, j in chunks:
-            add("T.%s.%d" % (blk, j), t_transpose(blk, j))
-            add("P.%s.%d" % (blk, j), t_copy(blk, j))
-            if blk[0] == "a":
-                add("Q.%s.%d" % (blk, j), t_quant_a(blk, j))
-            elif j == 3:
-                add("Q.%s" % blk, t_quant(blk))
-        for s in ("i", "h"):
-            for t in range(N_TILES):
-                for gb in range(N_BLOCKS):
-                    add("M.%s.%d.%d" % (s, t, gb), t_mx(s, t, gb))
-                    add("A.%s.%d.%d" % (s, t, gb), t_add(s, t, gb))
-                add("N.%s.%d" % (s, t), t_negmean(s, t))
-                if s == "h":
-                    add("K.%d" % t, t_nrh(t))
-                add("B.%s.%d" % (s, t), t_square(s, t))
-                if s == "i":
-                    if t % 4 == 3:
-                        add("R.i.%d" % (t // 4), t_rstd_i(t // 4))
-                else:
-                    add("R.h.%d" % t, t_rstd_h(t))
-                    add("U.%d" % t, t_shift(t))
-                    add("C.%d" % t, t_combine(t))
-                    for q in range(D_SPLIT.get(t, 1)):
-                        add("D.%d.%d" % (t, q), t_sigmoid(t, q))
-                        add("S.%d.%d" % (t, q), t_store(t, q))
+                nc.scalar.copy(out=dest, in_=src)
 
-        order = ORDER if ORDER else natural
-        assert sorted(order) == sorted(natural)
+        def w_transpose(s, b):
+            for c in range(4):
+                transpose(("w", s, b, c))
+
+        def w_regroup(s, b, chunks, on_vector):
+            if ("w", s, b) not in grouped:
+                grouped[("w", s, b)] = wq_pool.tile([P, 4 * PASSES * BANK], BF16, name="wq", align_bytes=64)
+            words = grouped[("w", s, b)][:].bitcast(F32).rearrange("q (g n u) -> q g n u", g=PASSES, n=BANK, u=2)
+            for c in chunks:
+                regroup(("w", s, b, c), words[:, :, c * P:(c + 1) * P, :], on_vector)
+
+        def w_quantise(s, b):
+            nc.vector.quantize_mx(
+                out=w_codes[s][:, b, :].bitcast(FP8X4), scales=w_scales[s][:, b, :], in_=grouped[("w", s, b)][:],
+            )
+
+        def a_transpose(j):
+            transpose(("a",) + JOBS[j])
+
+        def a_regroup(j):
+            key = ("a",) + JOBS[j]
+            grouped[key] = aq_pool.tile([P, 4 * WORDS], BF16, name="aq", align_bytes=64)
+            words = grouped[key][:].bitcast(F32).rearrange("q (g r u) -> q g r u", g=PASSES, r=P, u=2)
+            regroup(key, words, False)
+
+        def a_quantise(j):
+            s, t = JOBS[j]
+            nc.vector.quantize_mx(
+                out=a_codes[s][:, t, :].bitcast(FP8X4), scales=a_scales[s][:, t, :], in_=grouped[("a", s, t)][:],
+            )
+
+        def matmuls(j, blocks):
+            s, t = JOBS[j]
+            for b in blocks:
+                acc[(j, b)] = acc_psum.tile([P, BANK], F32, name="acc")
+                for g in range(PASSES):
+                    rows = slice(g * P, (g + 1) * P)
+                    cols = slice(g * BANK, (g + 1) * BANK)
+                    nc.tensor.matmul_mx(
+                        out=acc[(j, b)][:],
+                        lhsT=a_codes[s][:, t, rows].bitcast(FP8X4),
+                        lhsT_scale=a_scales[s][:, t, rows],
+                        rhs=w_codes[s][:, b, cols].bitcast(FP8X4),
+                        rhs_scale=w_scales[s][:, b, cols],
+                        start=(g == 0),
+                        stop=(g == PASSES - 1),
+                    )
+
+        def bias_add(j, blocks):
+            s, t = JOBS[j]
+            if j not in v:
+                v[j] = v_pool.tile([P, G], F32, name="v")
+            for b in blocks:
+                cols = slice(b * BANK, (b + 1) * BANK)
+                nc.vector.scalar_tensor_tensor(
+                    out=v[j][:, cols], in0=acc[(j, b)][:], scalar=1.0, in1=bias_bc[s][:, cols],
+                    op0=ALU.mult, op1=ALU.add, accum_out=bank_sum[s][:, t, b:b + 1],
+                )
+
+        def mean(j):
+            s, t = JOBS[j]
+            scaled = tiny.tile([P, N_BLOCKS], F32, name="scaled")
+            nc.scalar.activation(
+                out=scaled[:], in_=bank_sum[s][:, t, :], func=ACT.Identity, scale=-1.0 / G,
+                accum_out=neg_mean[s][:, t:t + 1],
+            )
+
+        def deviation(j):
+            s, t = JOBS[j]
+            one = slice(t, t + 1)
+            nc.scalar.activation(
+                out=squares_out[:], in_=v[j][:], func=ACT.Square, bias=neg_mean[s][:, one], scale=1.0,
+                accum_out=sq_dev[s][:, one],
+            )
+            var_eps = tiny.tile([P, 1], F32, name="var_eps")
+            nc.gpsimd.tensor_scalar(
+                out=var_eps[:], in0=sq_dev[s][:, one], scalar1=1.0 / G, scalar2=EPS, op0=ALU.mult, op1=ALU.add,
+            )
+            if s == "x":
+                nc.gpsimd.tensor_tensor(out=r_x[:, one], in0=var_eps[:], in1=neg_half[:], op=ALU.pow)
+                nc.gpsimd.tensor_tensor(out=s_x[:, one], in0=var_eps[:], in1=pos_half[:], op=ALU.pow)
+                nc.gpsimd.tensor_tensor(out=nr_x[:, one], in0=neg_mean[s][:, one], in1=r_x[:, one], op=ALU.mult)
+            else:
+                r_h = tiny.tile([P, 1], F32, name="r_h")
+                nc.gpsimd.tensor_tensor(out=r_h[:], in0=var_eps[:], in1=neg_half[:], op=ALU.pow)
+                nc.gpsimd.tensor_tensor(out=ratio[:, one], in0=r_h[:], in1=s_x[:, one], op=ALU.mult)
+                nc.gpsimd.tensor_scalar(
+                    out=shift[:, one], in0=r_h[:], scalar1=neg_mean[s][:, one], scalar2=nr_x[:, one],
+                    op0=ALU.mult, op1=ALU.add,
+                )
+
+        def combine(j):
+            t = JOBS[j][1]
+            nc.vector.scalar_tensor_tensor(
+                out=v[j][:], in0=v[j][:], scalar=ratio[:, t:t + 1], in1=v[t][:], op0=ALU.mult, op1=ALU.add,
+            )
+
+        def gate(j):
+            t = JOBS[j][1]
+            for half in range(HALVES):
+                cols = slice(half * G // HALVES, (half + 1) * G // HALVES)
+                nc.scalar.activation(
+                    out=v[j][:, cols], in_=v[j][:, cols], func=ACT.Sigmoid,
+                    bias=shift[:, t:t + 1], scale=r_x[:, t:t + 1],
+                )
+                nc.sync.dma_start(out=out[t * P:(t + 1) * P, cols], in_=v[j][:, cols])
+
+        def is_job(j, first=0):
+            return first <= j < N_JOBS
+
+        all_blocks = range(N_BLOCKS)
+
         with tc.manual_schedule():
-            for name in order:
-                emit(name, tasks[name])
+            for s in SIDES:
+                for b in all_blocks:
+                    for c in range(4):
+                        r0 = b * BANK + c * P
+                        load(("w", s, b, c), wgt_dram[s][r0:r0 + P, :])
+                    if b == 0:
+                        for t in range(EARLY):
+                            load(("a", s, t), act_dram[s][t * P:(t + 1) * P, :])
+                    cols = slice(b * BANK, (b + 1) * BANK)
+                    nc.sync.dma_start(out=bias_bc[s][:, cols], in_=bias_dram[s][cols].partition_broadcast(P))
+                for t in range(EARLY, N_TILES):
+                    load(("a", s, t), act_dram[s][t * P:(t + 1) * P, :])
+
+            for b in range(N_BLOCKS + 1):
+                if b < N_BLOCKS:
+                    w_transpose("x", b)
+                    w_regroup("x", b, range(4), False)
+                    w_quantise("x", b)
+                for j in range(EARLY):
+                    if b == 0:
+                        a_transpose(j)
+                        a_regroup(j)
+                        a_quantise(j)
+                    else:
+                        matmuls(j, [b - 1])
+                        bias_add(j, [b - 1])
+                if b == N_BLOCKS - 1:
+                    for j in range(EARLY, EARLY + 3):
+                        a_transpose(j)
+                        a_regroup(j)
+                    for j in range(EARLY, EARLY + 2):
+                        a_quantise(j)
+            matmuls(EARLY, all_blocks)
+            for j in range(EARLY):
+                mean(j)
+                if j < EARLY - 1:
+                    deviation(j)
+
+            for n in range(EARLY, N_JOBS + 3):
+                b = n - EARLY
+                if is_job(n + 3, EARLY + 3):
+                    a_transpose(n + 3)
+                if b < N_BLOCKS:
+                    w_transpose("h", b)
+                if is_job(n + 1):
+                    matmuls(n + 1, all_blocks)
+
+                if is_job(n):
+                    bias_add(n, all_blocks)
+                if 1 <= b <= N_BLOCKS:
+                    w_quantise("h", b - 1)
+                if is_job(n - 2, N_TILES):
+                    combine(n - 2)
+                if is_job(n + 2, EARLY + 2):
+                    a_quantise(n + 2)
+                if b < N_BLOCKS:
+                    w_regroup("h", b, [3], True)
+
+                if is_job(n - 1):
+                    deviation(n - 1)
+                if is_job(n + 3, EARLY + 3):
+                    a_regroup(n + 3)
+                if is_job(n):
+                    mean(n)
+                if b < N_BLOCKS:
+                    w_regroup("h", b, range(3), False)
+                if is_job(n - 3, N_TILES):
+                    gate(n - 3)

@@ -34,14 +34,13 @@ def tile_layernormgrucell_pa_kernel(tc, x, h, W_irz, b_irz, W_hrz, b_hrz, out):
     nc = tc.nc
     act_dram = {"x": x, "h": h}
     wgt_dram = {"x": W_irz, "h": W_hrz}
-    bias_dram = {"x": b_irz, "h": b_hrz}
 
     with ExitStack() as ctx:
         const = ctx.enter_context(tc.tile_pool(name="const", bufs=1))
         keep = ctx.enter_context(tc.tile_pool(name="keep", bufs=1))
         raw_pool = ctx.enter_context(tc.tile_pool(name="raw_pool", bufs=16))
         wq_pool = ctx.enter_context(tc.tile_pool(name="wq_pool", bufs=3))
-        aq_pool = ctx.enter_context(tc.tile_pool(name="aq_pool", bufs=6))
+        aq_pool = ctx.enter_context(tc.tile_pool(name="aq_pool", bufs=4))
         v_pool = ctx.enter_context(tc.tile_pool(name="v_pool", bufs=N_TILES + 3))
         tiny = ctx.enter_context(tc.tile_pool(name="tiny", bufs=4))
         tr_psum = ctx.enter_context(tc.psum_pool(name="tr_psum", bufs=5))
@@ -57,6 +56,11 @@ def tile_layernormgrucell_pa_kernel(tc, x, h, W_irz, b_irz, W_hrz, b_hrz, out):
         nc.vector.memset(warm_in[:], 0.0)
         warm_out = const.tile([P, 1], F32, name="warm_out")
         nc.scalar.activation(out=warm_out[:], in_=warm_in[:], func=ACT.Sigmoid)
+
+        ones = const.tile([P, P], BF16, name="ones")
+        nc.vector.memset(ones[:], 1.0)
+        bias_row = const.tile([P, G], BF16, name="bias_row")
+        nc.vector.memset(bias_row[:], 0.0)
 
         bias_bc = {}
         w_codes, w_scales, a_codes, a_scales = {}, {}, {}, {}
@@ -83,6 +87,8 @@ def tile_layernormgrucell_pa_kernel(tc, x, h, W_irz, b_irz, W_hrz, b_hrz, out):
         acc = {}
         v = {}
 
+        all_blocks = range(N_BLOCKS)
+
         def load(key, rows):
             raw[key] = raw_pool.tile([P, K], BF16, name="raw")
             nc.sync.dma_start(out=raw[key][:], in_=rows)
@@ -99,6 +105,12 @@ def tile_layernormgrucell_pa_kernel(tc, x, h, W_irz, b_irz, W_hrz, b_hrz, out):
                 nc.vector.tensor_copy(out=dest, in_=src)
             else:
                 nc.scalar.copy(out=dest, in_=src)
+
+        def spread_bias_x(b):
+            cols = slice(b * BANK, (b + 1) * BANK)
+            rep = acc_psum.tile([P, BANK], F32, name="acc")
+            nc.tensor.matmul(out=rep[:], lhsT=ones[:], rhs=bias_row[:, cols], start=True, stop=True)
+            nc.vector.tensor_copy(out=bias_bc["x"][:, cols], in_=rep[:])
 
         def w_transpose(s, b):
             for c in range(4):
@@ -210,8 +222,6 @@ def tile_layernormgrucell_pa_kernel(tc, x, h, W_irz, b_irz, W_hrz, b_hrz, out):
         def is_job(j, first=0):
             return first <= j < N_JOBS
 
-        all_blocks = range(N_BLOCKS)
-
         with tc.manual_schedule():
             for s in SIDES:
                 for b in all_blocks:
@@ -219,16 +229,19 @@ def tile_layernormgrucell_pa_kernel(tc, x, h, W_irz, b_irz, W_hrz, b_hrz, out):
                         r0 = b * BANK + c * P
                         load(("w", s, b, c), wgt_dram[s][r0:r0 + P, :])
                     if b == 0:
+                        if s == "x":
+                            nc.sync.dma_start(out=bias_row[0:1, :], in_=b_irz.unsqueeze(0))
                         for t in range(EARLY):
                             load(("a", s, t), act_dram[s][t * P:(t + 1) * P, :])
-                    cols = slice(b * BANK, (b + 1) * BANK)
-                    nc.sync.dma_start(out=bias_bc[s][:, cols], in_=bias_dram[s][cols].partition_broadcast(P))
+                if s == "h":
+                    nc.sync.dma_start(out=bias_bc["h"][:], in_=b_hrz.partition_broadcast(P))
                 for t in range(EARLY, N_TILES):
                     load(("a", s, t), act_dram[s][t * P:(t + 1) * P, :])
 
             for b in range(N_BLOCKS + 1):
                 if b < N_BLOCKS:
                     w_transpose("x", b)
+                    spread_bias_x(b)
                     w_regroup("x", b, range(4), False)
                     w_quantise("x", b)
                 for j in range(EARLY):

@@ -39,7 +39,7 @@ def tile_layernormgrucell_pa_kernel(tc, x, h, W_irz, b_irz, W_hrz, b_hrz, out):
         const = ctx.enter_context(tc.tile_pool(name="const", bufs=1))
         keep = ctx.enter_context(tc.tile_pool(name="keep", bufs=1))
         raw_pool = ctx.enter_context(tc.tile_pool(name="raw_pool", bufs=16))
-        wq_pool = ctx.enter_context(tc.tile_pool(name="wq_pool", bufs=3))
+        wq_pool = ctx.enter_context(tc.tile_pool(name="wq_pool", bufs=2))
         aq_pool = ctx.enter_context(tc.tile_pool(name="aq_pool", bufs=4))
         v_pool = ctx.enter_context(tc.tile_pool(name="v_pool", bufs=N_TILES + 3))
         tiny = ctx.enter_context(tc.tile_pool(name="tiny", bufs=4))
@@ -59,8 +59,10 @@ def tile_layernormgrucell_pa_kernel(tc, x, h, W_irz, b_irz, W_hrz, b_hrz, out):
 
         ones = const.tile([P, P], BF16, name="ones")
         nc.vector.memset(ones[:], 1.0)
-        bias_row = const.tile([P, G], BF16, name="bias_row")
-        nc.vector.memset(bias_row[:], 0.0)
+        bias_row = {}
+        for s in SIDES:
+            bias_row[s] = const.tile([P, G], BF16, name="bias_row_%s" % s)
+            nc.vector.memset(bias_row[s][:], 0.0)
 
         bias_bc = {}
         w_codes, w_scales, a_codes, a_scales = {}, {}, {}, {}
@@ -106,11 +108,11 @@ def tile_layernormgrucell_pa_kernel(tc, x, h, W_irz, b_irz, W_hrz, b_hrz, out):
             else:
                 nc.scalar.copy(out=dest, in_=src)
 
-        def spread_bias_x(b):
+        def spread_bias(s, b):
             cols = slice(b * BANK, (b + 1) * BANK)
             rep = acc_psum.tile([P, BANK], F32, name="acc")
-            nc.tensor.matmul(out=rep[:], lhsT=ones[:], rhs=bias_row[:, cols], start=True, stop=True)
-            nc.vector.tensor_copy(out=bias_bc["x"][:, cols], in_=rep[:])
+            nc.tensor.matmul(out=rep[:], lhsT=ones[:], rhs=bias_row[s][:, cols], start=True, stop=True)
+            nc.vector.tensor_copy(out=bias_bc[s][:, cols], in_=rep[:])
 
         def w_transpose(s, b):
             for c in range(4):
@@ -230,18 +232,18 @@ def tile_layernormgrucell_pa_kernel(tc, x, h, W_irz, b_irz, W_hrz, b_hrz, out):
                         load(("w", s, b, c), wgt_dram[s][r0:r0 + P, :])
                     if b == 0:
                         if s == "x":
-                            nc.sync.dma_start(out=bias_row[0:1, :], in_=b_irz.unsqueeze(0))
+                            nc.sync.dma_start(out=bias_row["x"][0:1, :], in_=b_irz.unsqueeze(0))
+                            nc.sync.dma_start(out=bias_row["h"][0:1, :], in_=b_hrz.unsqueeze(0))
                         for t in range(EARLY):
                             load(("a", s, t), act_dram[s][t * P:(t + 1) * P, :])
-                if s == "h":
-                    nc.sync.dma_start(out=bias_bc["h"][:], in_=b_hrz.partition_broadcast(P))
                 for t in range(EARLY, N_TILES):
                     load(("a", s, t), act_dram[s][t * P:(t + 1) * P, :])
 
             for b in range(N_BLOCKS + 1):
                 if b < N_BLOCKS:
                     w_transpose("x", b)
-                    spread_bias_x(b)
+                    for s in SIDES:
+                        spread_bias(s, b)
                     w_regroup("x", b, range(4), False)
                     w_quantise("x", b)
                 for j in range(EARLY):

@@ -27,6 +27,7 @@ SIDES = ("x", "h")
 JOBS = tuple((side, t) for side in SIDES for t in range(N_TILES))
 N_JOBS = len(JOBS)
 EARLY = 2
+B_H_STEP = 4
 HALVES = 2
 
 
@@ -39,7 +40,7 @@ def tile_layernormgrucell_pa_kernel(tc, x, h, W_irz, b_irz, W_hrz, b_hrz, out):
         const = ctx.enter_context(tc.tile_pool(name="const", bufs=1))
         keep = ctx.enter_context(tc.tile_pool(name="keep", bufs=1))
         raw_pool = ctx.enter_context(tc.tile_pool(name="raw_pool", bufs=16))
-        wq_pool = ctx.enter_context(tc.tile_pool(name="wq_pool", bufs=2))
+        wq_pool = ctx.enter_context(tc.tile_pool(name="wq_pool", bufs=3))
         aq_pool = ctx.enter_context(tc.tile_pool(name="aq_pool", bufs=4))
         v_pool = ctx.enter_context(tc.tile_pool(name="v_pool", bufs=N_TILES + 3))
         tiny = ctx.enter_context(tc.tile_pool(name="tiny", bufs=4))
@@ -59,10 +60,8 @@ def tile_layernormgrucell_pa_kernel(tc, x, h, W_irz, b_irz, W_hrz, b_hrz, out):
 
         ones = const.tile([P, P], BF16, name="ones")
         nc.vector.memset(ones[:], 1.0)
-        bias_row = {}
-        for s in SIDES:
-            bias_row[s] = const.tile([P, G], BF16, name="bias_row_%s" % s)
-            nc.vector.memset(bias_row[s][:], 0.0)
+        bias_row = const.tile([P, G], BF16, name="bias_row")
+        nc.vector.memset(bias_row[:], 0.0)
 
         bias_bc = {}
         w_codes, w_scales, a_codes, a_scales = {}, {}, {}, {}
@@ -108,11 +107,11 @@ def tile_layernormgrucell_pa_kernel(tc, x, h, W_irz, b_irz, W_hrz, b_hrz, out):
             else:
                 nc.scalar.copy(out=dest, in_=src)
 
-        def spread_bias(s, b):
+        def spread_bias_x(b):
             cols = slice(b * BANK, (b + 1) * BANK)
             rep = acc_psum.tile([P, BANK], F32, name="acc")
-            nc.tensor.matmul(out=rep[:], lhsT=ones[:], rhs=bias_row[s][:, cols], start=True, stop=True)
-            nc.vector.tensor_copy(out=bias_bc[s][:, cols], in_=rep[:])
+            nc.tensor.matmul(out=rep[:], lhsT=ones[:], rhs=bias_row[:, cols], start=True, stop=True)
+            nc.vector.tensor_copy(out=bias_bc["x"][:, cols], in_=rep[:])
 
         def w_transpose(s, b):
             for c in range(4):
@@ -232,8 +231,7 @@ def tile_layernormgrucell_pa_kernel(tc, x, h, W_irz, b_irz, W_hrz, b_hrz, out):
                         load(("w", s, b, c), wgt_dram[s][r0:r0 + P, :])
                     if b == 0:
                         if s == "x":
-                            nc.sync.dma_start(out=bias_row["x"][0:1, :], in_=b_irz.unsqueeze(0))
-                            nc.sync.dma_start(out=bias_row["h"][0:1, :], in_=b_hrz.unsqueeze(0))
+                            nc.sync.dma_start(out=bias_row[0:1, :], in_=b_irz.unsqueeze(0))
                         for t in range(EARLY):
                             load(("a", s, t), act_dram[s][t * P:(t + 1) * P, :])
                 for t in range(EARLY, N_TILES):
@@ -242,8 +240,7 @@ def tile_layernormgrucell_pa_kernel(tc, x, h, W_irz, b_irz, W_hrz, b_hrz, out):
             for b in range(N_BLOCKS + 1):
                 if b < N_BLOCKS:
                     w_transpose("x", b)
-                    for s in SIDES:
-                        spread_bias(s, b)
+                    spread_bias_x(b)
                     w_regroup("x", b, range(4), False)
                     w_quantise("x", b)
                 for j in range(EARLY):
@@ -288,6 +285,8 @@ def tile_layernormgrucell_pa_kernel(tc, x, h, W_irz, b_irz, W_hrz, b_hrz, out):
 
                 if is_job(n - 1):
                     deviation(n - 1)
+                if n == B_H_STEP:
+                    nc.gpsimd.dma_start(out=bias_bc["h"][:], in_=b_hrz.partition_broadcast(P))
                 if is_job(n + 3, EARLY + 3):
                     a_regroup(n + 3)
                 if is_job(n):

@@ -26,8 +26,8 @@ FLOPS = 2 * 2 * B * K * G
 SIDES = ("x", "h")
 JOBS = tuple((side, t) for side in SIDES for t in range(N_TILES))
 N_JOBS = len(JOBS)
-EARLY = 2
-B_H_STEP = 4
+LEAD = 5
+W_H_STEP = 2
 HALVES = 2
 
 
@@ -39,8 +39,8 @@ def tile_layernormgrucell_pa_kernel(tc, x, h, W_irz, b_irz, W_hrz, b_hrz, out):
     with ExitStack() as ctx:
         const = ctx.enter_context(tc.tile_pool(name="const", bufs=1))
         keep = ctx.enter_context(tc.tile_pool(name="keep", bufs=1))
-        raw_pool = ctx.enter_context(tc.tile_pool(name="raw_pool", bufs=16))
-        wq_pool = ctx.enter_context(tc.tile_pool(name="wq_pool", bufs=3))
+        raw_pool = ctx.enter_context(tc.tile_pool(name="raw_pool", bufs=18))
+        wq_pool = ctx.enter_context(tc.tile_pool(name="wq_pool", bufs=2))
         aq_pool = ctx.enter_context(tc.tile_pool(name="aq_pool", bufs=4))
         v_pool = ctx.enter_context(tc.tile_pool(name="v_pool", bufs=N_TILES + 3))
         tiny = ctx.enter_context(tc.tile_pool(name="tiny", bufs=4))
@@ -60,8 +60,10 @@ def tile_layernormgrucell_pa_kernel(tc, x, h, W_irz, b_irz, W_hrz, b_hrz, out):
 
         ones = const.tile([P, P], BF16, name="ones")
         nc.vector.memset(ones[:], 1.0)
-        bias_row = const.tile([P, G], BF16, name="bias_row")
-        nc.vector.memset(bias_row[:], 0.0)
+        bias_row = {}
+        for s in SIDES:
+            bias_row[s] = const.tile([P, G], BF16, name="bias_row_%s" % s)
+            nc.vector.memset(bias_row[s][:], 0.0)
 
         bias_bc = {}
         w_codes, w_scales, a_codes, a_scales = {}, {}, {}, {}
@@ -107,11 +109,11 @@ def tile_layernormgrucell_pa_kernel(tc, x, h, W_irz, b_irz, W_hrz, b_hrz, out):
             else:
                 nc.scalar.copy(out=dest, in_=src)
 
-        def spread_bias_x(b):
+        def spread_bias(s, b):
             cols = slice(b * BANK, (b + 1) * BANK)
             rep = acc_psum.tile([P, BANK], F32, name="acc")
-            nc.tensor.matmul(out=rep[:], lhsT=ones[:], rhs=bias_row[:, cols], start=True, stop=True)
-            nc.vector.tensor_copy(out=bias_bc["x"][:, cols], in_=rep[:])
+            nc.tensor.matmul(out=rep[:], lhsT=ones[:], rhs=bias_row[s][:, cols], start=True, stop=True)
+            nc.vector.tensor_copy(out=bias_bc[s][:, cols], in_=rep[:])
 
         def w_transpose(s, b):
             for c in range(4):
@@ -229,45 +231,24 @@ def tile_layernormgrucell_pa_kernel(tc, x, h, W_irz, b_irz, W_hrz, b_hrz, out):
                     for c in range(4):
                         r0 = b * BANK + c * P
                         load(("w", s, b, c), wgt_dram[s][r0:r0 + P, :])
-                    if b == 0:
-                        if s == "x":
-                            nc.sync.dma_start(out=bias_row[0:1, :], in_=b_irz.unsqueeze(0))
-                        for t in range(EARLY):
-                            load(("a", s, t), act_dram[s][t * P:(t + 1) * P, :])
-                for t in range(EARLY, N_TILES):
+                    if b == 0 and s == "x":
+                        nc.sync.dma_start(out=bias_row["x"][0:1, :], in_=b_irz.unsqueeze(0))
+                        nc.sync.dma_start(out=bias_row["h"][0:1, :], in_=b_hrz.unsqueeze(0))
+                for t in range(N_TILES):
                     load(("a", s, t), act_dram[s][t * P:(t + 1) * P, :])
 
-            for b in range(N_BLOCKS + 1):
-                if b < N_BLOCKS:
-                    w_transpose("x", b)
-                    spread_bias_x(b)
-                    w_regroup("x", b, range(4), False)
-                    w_quantise("x", b)
-                for j in range(EARLY):
-                    if b == 0:
-                        a_transpose(j)
-                        a_regroup(j)
-                        a_quantise(j)
-                    else:
-                        matmuls(j, [b - 1])
-                        bias_add(j, [b - 1])
-                if b == N_BLOCKS - 1:
-                    for j in range(EARLY, EARLY + 3):
-                        a_transpose(j)
-                        a_regroup(j)
-                    for j in range(EARLY, EARLY + 2):
-                        a_quantise(j)
-            matmuls(EARLY, all_blocks)
-            for j in range(EARLY):
-                mean(j)
-                if j < EARLY - 1:
-                    deviation(j)
+            for b in all_blocks:
+                w_transpose("x", b)
+                for s in SIDES:
+                    spread_bias(s, b)
+                w_regroup("x", b, range(4), False)
+                w_quantise("x", b)
 
-            for n in range(EARLY, N_JOBS + 3):
-                b = n - EARLY
-                if is_job(n + 3, EARLY + 3):
-                    a_transpose(n + 3)
-                if b < N_BLOCKS:
+            for n in range(-LEAD, N_JOBS + 3):
+                b = n - W_H_STEP
+                if is_job(n + LEAD):
+                    a_transpose(n + LEAD)
+                if 0 <= b < N_BLOCKS:
                     w_transpose("h", b)
                 if is_job(n + 1):
                     matmuls(n + 1, all_blocks)
@@ -278,20 +259,16 @@ def tile_layernormgrucell_pa_kernel(tc, x, h, W_irz, b_irz, W_hrz, b_hrz, out):
                     w_quantise("h", b - 1)
                 if is_job(n - 2, N_TILES):
                     combine(n - 2)
-                if is_job(n + 2, EARLY + 2):
-                    a_quantise(n + 2)
-                if b < N_BLOCKS:
-                    w_regroup("h", b, [3], True)
+                if is_job(n + LEAD - 1):
+                    a_quantise(n + LEAD - 1)
 
                 if is_job(n - 1):
                     deviation(n - 1)
-                if n == B_H_STEP:
-                    nc.gpsimd.dma_start(out=bias_bc["h"][:], in_=b_hrz.partition_broadcast(P))
-                if is_job(n + 3, EARLY + 3):
-                    a_regroup(n + 3)
+                if is_job(n + LEAD):
+                    a_regroup(n + LEAD)
                 if is_job(n):
                     mean(n)
-                if b < N_BLOCKS:
-                    w_regroup("h", b, range(3), False)
+                if 0 <= b < N_BLOCKS:
+                    w_regroup("h", b, range(4), False)
                 if is_job(n - 3, N_TILES):
                     gate(n - 3)

@@ -26,8 +26,7 @@ FLOPS = 2 * 2 * B * K * G
 SIDES = ("x", "h")
 JOBS = tuple((side, t) for side in SIDES for t in range(N_TILES))
 N_JOBS = len(JOBS)
-LEAD = 5
-W_H_STEP = 2
+EARLY = 2
 HALVES = 2
 
 
@@ -39,7 +38,7 @@ def tile_layernormgrucell_pa_kernel(tc, x, h, W_irz, b_irz, W_hrz, b_hrz, out):
     with ExitStack() as ctx:
         const = ctx.enter_context(tc.tile_pool(name="const", bufs=1))
         keep = ctx.enter_context(tc.tile_pool(name="keep", bufs=1))
-        raw_pool = ctx.enter_context(tc.tile_pool(name="raw_pool", bufs=18))
+        raw_pool = ctx.enter_context(tc.tile_pool(name="raw_pool", bufs=20))
         wq_pool = ctx.enter_context(tc.tile_pool(name="wq_pool", bufs=2))
         aq_pool = ctx.enter_context(tc.tile_pool(name="aq_pool", bufs=4))
         v_pool = ctx.enter_context(tc.tile_pool(name="v_pool", bufs=N_TILES + 3))
@@ -231,24 +230,47 @@ def tile_layernormgrucell_pa_kernel(tc, x, h, W_irz, b_irz, W_hrz, b_hrz, out):
                     for c in range(4):
                         r0 = b * BANK + c * P
                         load(("w", s, b, c), wgt_dram[s][r0:r0 + P, :])
-                    if b == 0 and s == "x":
-                        nc.sync.dma_start(out=bias_row["x"][0:1, :], in_=b_irz.unsqueeze(0))
-                        nc.sync.dma_start(out=bias_row["h"][0:1, :], in_=b_hrz.unsqueeze(0))
-                for t in range(N_TILES):
+                    if b == 0:
+                        if s == "x":
+                            nc.sync.dma_start(out=bias_row["x"][0:1, :], in_=b_irz.unsqueeze(0))
+                            nc.sync.dma_start(out=bias_row["h"][0:1, :], in_=b_hrz.unsqueeze(0))
+                        for t in range(EARLY):
+                            load(("a", s, t), act_dram[s][t * P:(t + 1) * P, :])
+                for t in range(EARLY, N_TILES):
                     load(("a", s, t), act_dram[s][t * P:(t + 1) * P, :])
 
-            for b in all_blocks:
-                w_transpose("x", b)
-                for s in SIDES:
-                    spread_bias(s, b)
-                w_regroup("x", b, range(4), False)
-                w_quantise("x", b)
+            for b in range(N_BLOCKS + 1):
+                if b < N_BLOCKS:
+                    w_transpose("x", b)
+                    for s in SIDES:
+                        spread_bias(s, b)
+                    w_regroup("x", b, range(4), False)
+                    w_quantise("x", b)
+                for j in range(EARLY):
+                    if b == 0:
+                        a_transpose(j)
+                        a_regroup(j)
+                        a_quantise(j)
+                    else:
+                        matmuls(j, [b - 1])
+                        bias_add(j, [b - 1])
+                if b == N_BLOCKS - 1:
+                    for j in range(EARLY, EARLY + 3):
+                        a_transpose(j)
+                        a_regroup(j)
+                    for j in range(EARLY, EARLY + 2):
+                        a_quantise(j)
+            matmuls(EARLY, all_blocks)
+            for j in range(EARLY):
+                mean(j)
+                if j < EARLY - 1:
+                    deviation(j)
 
-            for n in range(-LEAD, N_JOBS + 3):
-                b = n - W_H_STEP
-                if is_job(n + LEAD):
-                    a_transpose(n + LEAD)
-                if 0 <= b < N_BLOCKS:
+            for n in range(EARLY, N_JOBS + 3):
+                b = n - EARLY
+                if is_job(n + 3, EARLY + 3):
+                    a_transpose(n + 3)
+                if b < N_BLOCKS:
                     w_transpose("h", b)
                 if is_job(n + 1):
                     matmuls(n + 1, all_blocks)
@@ -259,16 +281,18 @@ def tile_layernormgrucell_pa_kernel(tc, x, h, W_irz, b_irz, W_hrz, b_hrz, out):
                     w_quantise("h", b - 1)
                 if is_job(n - 2, N_TILES):
                     combine(n - 2)
-                if is_job(n + LEAD - 1):
-                    a_quantise(n + LEAD - 1)
+                if is_job(n + 2, EARLY + 2):
+                    a_quantise(n + 2)
+                if b < N_BLOCKS:
+                    w_regroup("h", b, [3], True)
 
                 if is_job(n - 1):
                     deviation(n - 1)
-                if is_job(n + LEAD):
-                    a_regroup(n + LEAD)
+                if is_job(n + 3, EARLY + 3):
+                    a_regroup(n + 3)
                 if is_job(n):
                     mean(n)
-                if 0 <= b < N_BLOCKS:
-                    w_regroup("h", b, range(4), False)
+                if b < N_BLOCKS:
+                    w_regroup("h", b, range(3), False)
                 if is_job(n - 3, N_TILES):
                     gate(n - 3)

@@ -26,6 +26,16 @@ FLOPS = 2 * 2 * B * K * G
 SIDES = ("x", "h")
 JOBS = tuple((side, t) for side in SIDES for t in range(N_TILES))
 N_JOBS = len(JOBS)
+WARM = 0
+HS = 6
+HV = ((3,), (3,), (), ())
+XV = ((), (), (), ())
+VX = "eaqv"
+VH = "eac"
+SX = "amwd"
+SH = "dfgma"
+CL, GL, DL = 2, 3, 1
+TQ = 4
 EARLY = 2
 HALVES = 2
 
@@ -48,9 +58,9 @@ def tile_layernormgrucell_pa_kernel(tc, x, h, W_irz, b_irz, W_hrz, b_hrz, out):
 
         ident = const.tile([P, P], F32, name="ident")
         make_identity(nc, ident[:])
-        neg_half = const.tile([P, 1], F32, name="neg_half")
+        neg_half = const.tile([P, N_TILES], F32, name="neg_half")
         nc.gpsimd.memset(neg_half[:], -0.5)
-        pos_half = const.tile([P, 1], F32, name="pos_half")
+        pos_half = const.tile([P, N_TILES], F32, name="pos_half")
         nc.gpsimd.memset(pos_half[:], 0.5)
         warm_in = const.tile([P, 1], F32, name="warm_in")
         nc.vector.memset(warm_in[:], 0.0)
@@ -62,7 +72,10 @@ def tile_layernormgrucell_pa_kernel(tc, x, h, W_irz, b_irz, W_hrz, b_hrz, out):
         bias_row = {}
         for s in SIDES:
             bias_row[s] = const.tile([P, G], BF16, name="bias_row_%s" % s)
-            nc.vector.memset(bias_row[s][:], 0.0)
+            nc.vector.memset(bias_row[s][:].bitcast(U32), 0)
+        warm_rhs = const.tile([P, BANK], BF16, name="warm_rhs")
+        if WARM:
+            nc.vector.memset(warm_rhs[:], 0.0)
 
         bias_bc = {}
         w_codes, w_scales, a_codes, a_scales = {}, {}, {}, {}
@@ -108,11 +121,19 @@ def tile_layernormgrucell_pa_kernel(tc, x, h, W_irz, b_irz, W_hrz, b_hrz, out):
             else:
                 nc.scalar.copy(out=dest, in_=src)
 
-        def spread_bias(s, b):
-            cols = slice(b * BANK, (b + 1) * BANK)
-            rep = acc_psum.tile([P, BANK], F32, name="acc")
-            nc.tensor.matmul(out=rep[:], lhsT=ones[:], rhs=bias_row[s][:, cols], start=True, stop=True)
-            nc.vector.tensor_copy(out=bias_bc[s][:, cols], in_=rep[:])
+        spread = {}
+
+        def spread_matmul(s, half):
+            rep = spread[(s, half)] = tr_psum.tile([P, 2 * BANK], BF16, name="turned")
+            for i in range(2):
+                c0 = (2 * half + i) * BANK
+                nc.tensor.matmul(
+                    out=rep[:, i * BANK:(i + 1) * BANK], lhsT=ones[:], rhs=bias_row[s][:, c0:c0 + BANK],
+                    start=True, stop=True,
+                )
+
+        def spread_copy(s, half):
+            nc.vector.tensor_copy(out=bias_bc[s][:, 2 * half * BANK:(2 * half + 2) * BANK], in_=spread[(s, half)][:])
 
         def w_transpose(s, b):
             for c in range(4):
@@ -188,33 +209,44 @@ def tile_layernormgrucell_pa_kernel(tc, x, h, W_irz, b_irz, W_hrz, b_hrz, out):
                 out=squares_out[:], in_=v[j][:], func=ACT.Square, bias=neg_mean[s][:, one], scale=1.0,
                 accum_out=sq_dev[s][:, one],
             )
+            if s == "x":
+                return
             var_eps = tiny.tile([P, 1], F32, name="var_eps")
             nc.gpsimd.tensor_scalar(
                 out=var_eps[:], in0=sq_dev[s][:, one], scalar1=1.0 / G, scalar2=EPS, op0=ALU.mult, op1=ALU.add,
             )
-            if s == "x":
-                nc.gpsimd.tensor_tensor(out=r_x[:, one], in0=var_eps[:], in1=neg_half[:], op=ALU.pow)
-                nc.gpsimd.tensor_tensor(out=s_x[:, one], in0=var_eps[:], in1=pos_half[:], op=ALU.pow)
-                nc.gpsimd.tensor_tensor(out=nr_x[:, one], in0=neg_mean[s][:, one], in1=r_x[:, one], op=ALU.mult)
-            else:
-                r_h = tiny.tile([P, 1], F32, name="r_h")
-                nc.gpsimd.tensor_tensor(out=r_h[:], in0=var_eps[:], in1=neg_half[:], op=ALU.pow)
-                nc.gpsimd.tensor_tensor(out=ratio[:, one], in0=r_h[:], in1=s_x[:, one], op=ALU.mult)
-                nc.gpsimd.tensor_scalar(
-                    out=shift[:, one], in0=r_h[:], scalar1=neg_mean[s][:, one], scalar2=nr_x[:, one],
-                    op0=ALU.mult, op1=ALU.add,
-                )
+            r_h = tiny.tile([P, 1], F32, name="r_h")
+            nc.gpsimd.tensor_tensor(out=r_h[:], in0=var_eps[:], in1=neg_half[:, 0:1], op=ALU.pow)
+            nc.gpsimd.tensor_tensor(out=ratio[:, one], in0=r_h[:], in1=s_x[:, one], op=ALU.mult)
+            nc.gpsimd.tensor_scalar(
+                out=shift[:, one], in0=r_h[:], scalar1=neg_mean[s][:, one], scalar2=nr_x[:, one],
+                op0=ALU.mult, op1=ALU.add,
+            )
+
+        def x_factors():
+            var_eps_x = keep.tile([P, N_TILES], F32, name="var_eps_x")
+            nc.gpsimd.tensor_scalar(
+                out=var_eps_x[:], in0=sq_dev["x"][:], scalar1=1.0 / G, scalar2=EPS, op0=ALU.mult, op1=ALU.add,
+            )
+            nc.gpsimd.tensor_tensor(out=r_x[:], in0=var_eps_x[:], in1=neg_half[:], op=ALU.pow)
+            nc.gpsimd.tensor_tensor(out=s_x[:], in0=var_eps_x[:], in1=pos_half[:], op=ALU.pow)
+            nc.gpsimd.tensor_tensor(out=nr_x[:], in0=neg_mean["x"][:], in1=r_x[:], op=ALU.mult)
 
         def combine(j):
             t = JOBS[j][1]
-            nc.vector.scalar_tensor_tensor(
-                out=v[j][:], in0=v[j][:], scalar=ratio[:, t:t + 1], in1=v[t][:], op0=ALU.mult, op1=ALU.add,
-            )
+            n_pieces = TQ if j == N_JOBS - 1 else 1
+            for i in range(n_pieces):
+                cols = slice(i * G // n_pieces, (i + 1) * G // n_pieces)
+                nc.vector.scalar_tensor_tensor(
+                    out=v[j][:, cols], in0=v[j][:, cols], scalar=ratio[:, t:t + 1], in1=v[t][:, cols],
+                    op0=ALU.mult, op1=ALU.add,
+                )
 
         def gate(j):
             t = JOBS[j][1]
-            for half in range(HALVES):
-                cols = slice(half * G // HALVES, (half + 1) * G // HALVES)
+            n_pieces = TQ if j == N_JOBS - 1 else HALVES
+            for i in range(n_pieces):
+                cols = slice(i * G // n_pieces, (i + 1) * G // n_pieces)
                 nc.scalar.activation(
                     out=v[j][:, cols], in_=v[j][:, cols], func=ACT.Sigmoid,
                     bias=shift[:, t:t + 1], scale=r_x[:, t:t + 1],
@@ -239,12 +271,17 @@ def tile_layernormgrucell_pa_kernel(tc, x, h, W_irz, b_irz, W_hrz, b_hrz, out):
                 for t in range(EARLY, N_TILES):
                     load(("a", s, t), act_dram[s][t * P:(t + 1) * P, :])
 
+            for i in range(WARM):
+                warm_bank = tr_psum.tile([P, BANK], F32, name="turned")
+                nc.tensor.matmul(out=warm_bank[:], lhsT=ones[:], rhs=warm_rhs[:], start=True, stop=True)
             for b in range(N_BLOCKS + 1):
                 if b < N_BLOCKS:
                     w_transpose("x", b)
-                    for s in SIDES:
-                        spread_bias(s, b)
-                    w_regroup("x", b, range(4), False)
+                    w_regroup("x", b, [c for c in range(4) if c not in XV[b]], False)
+                    w_regroup("x", b, XV[b], True)
+                    if b < 2:
+                        spread_matmul("x", b)
+                        spread_copy("x", b)
                     w_quantise("x", b)
                 for j in range(EARLY):
                     if b == 0:
@@ -263,36 +300,42 @@ def tile_layernormgrucell_pa_kernel(tc, x, h, W_irz, b_irz, W_hrz, b_hrz, out):
             matmuls(EARLY, all_blocks)
             for j in range(EARLY):
                 mean(j)
-                if j < EARLY - 1:
+                if j < EARLY - DL:
                     deviation(j)
-
-            for n in range(EARLY, N_JOBS + 3):
+            for n in range(EARLY, N_JOBS + GL):
                 b = n - EARLY
                 if is_job(n + 3, EARLY + 3):
                     a_transpose(n + 3)
                 if b < N_BLOCKS:
                     w_transpose("h", b)
+                if HS <= n < HS + 2:
+                    spread_matmul("h", n - HS)
                 if is_job(n + 1):
                     matmuls(n + 1, all_blocks)
-
-                if is_job(n):
-                    bias_add(n, all_blocks)
-                if 1 <= b <= N_BLOCKS:
-                    w_quantise("h", b - 1)
-                if is_job(n - 2, N_TILES):
-                    combine(n - 2)
-                if is_job(n + 2, EARLY + 2):
-                    a_quantise(n + 2)
-                if b < N_BLOCKS:
-                    w_regroup("h", b, [3], True)
-
-                if is_job(n - 1):
-                    deviation(n - 1)
-                if is_job(n + 3, EARLY + 3):
-                    a_regroup(n + 3)
-                if is_job(n):
-                    mean(n)
-                if b < N_BLOCKS:
-                    w_regroup("h", b, range(3), False)
-                if is_job(n - 3, N_TILES):
-                    gate(n - 3)
+                for o in (VX if n < N_TILES else VH):
+                    if o == "e" and is_job(n):
+                        bias_add(n, all_blocks)
+                    if o == "q" and 1 <= b <= N_BLOCKS:
+                        w_quantise("h", b - 1)
+                    if o == "c" and is_job(n - CL, N_TILES):
+                        combine(n - CL)
+                    if o == "a" and is_job(n + 2, EARLY + 2):
+                        a_quantise(n + 2)
+                    if o == "v":
+                        if b < N_BLOCKS:
+                            w_regroup("h", b, HV[b], True)
+                        if HS <= n < HS + 2:
+                            spread_copy("h", n - HS)
+                for o in (SX if n < N_TILES else SH):
+                    if o == "d" and is_job(n - DL):
+                        deviation(n - DL)
+                    if o == "f" and n == N_TILES + DL - 1:
+                        x_factors()
+                    if o == "a" and is_job(n + 3, EARLY + 3):
+                        a_regroup(n + 3)
+                    if o == "m" and is_job(n):
+                        mean(n)
+                    if o == "w" and b < N_BLOCKS:
+                        w_regroup("h", b, [c for c in range(4) if c not in HV[b]], False)
+                    if o == "g" and is_job(n - GL, N_TILES):
+                        gate(n - GL)

@@ -26,18 +26,23 @@ FLOPS = 2 * 2 * B * K * G
 SIDES = ("x", "h")
 JOBS = tuple((side, t) for side in SIDES for t in range(N_TILES))
 N_JOBS = len(JOBS)
+EARLY = 2
 WARM = 0
+PAIRS = 0
+SG = 1
+BHDMA = 1
 HS = 6
-HV = ((3,), (3,), (), ())
+HV = ((3,), (3,), (3,), (3,))
 XV = ((), (), (), ())
 VX = "eaqv"
-VH = "eac"
-SX = "amwd"
-SH = "dfgma"
-CL, GL, DL = 2, 3, 1
-TQ = 4
-EARLY = 2
+VH = "erac"
+SX = "awdm"
+SH = "dgmat"
+CL, GL = 2, 3
+TQ = 2
 HALVES = 2
+BATCH = 4
+AV = (13, 15)
 
 
 def tile_layernormgrucell_pa_kernel(tc, x, h, W_irz, b_irz, W_hrz, b_hrz, out):
@@ -48,20 +53,17 @@ def tile_layernormgrucell_pa_kernel(tc, x, h, W_irz, b_irz, W_hrz, b_hrz, out):
     with ExitStack() as ctx:
         const = ctx.enter_context(tc.tile_pool(name="const", bufs=1))
         keep = ctx.enter_context(tc.tile_pool(name="keep", bufs=1))
-        raw_pool = ctx.enter_context(tc.tile_pool(name="raw_pool", bufs=20))
+        raw_pool = ctx.enter_context(tc.tile_pool(name="raw_pool", bufs=6))
         wq_pool = ctx.enter_context(tc.tile_pool(name="wq_pool", bufs=2))
         aq_pool = ctx.enter_context(tc.tile_pool(name="aq_pool", bufs=4))
         v_pool = ctx.enter_context(tc.tile_pool(name="v_pool", bufs=N_TILES + 3))
         tiny = ctx.enter_context(tc.tile_pool(name="tiny", bufs=4))
-        tr_psum = ctx.enter_context(tc.psum_pool(name="tr_psum", bufs=5))
-        acc_psum = ctx.enter_context(tc.psum_pool(name="acc_psum", bufs=3))
+        psum = ctx.enter_context(tc.psum_pool(name="psum", bufs=8))
 
         ident = const.tile([P, P], F32, name="ident")
         make_identity(nc, ident[:])
         neg_half = const.tile([P, N_TILES], F32, name="neg_half")
         nc.gpsimd.memset(neg_half[:], -0.5)
-        pos_half = const.tile([P, N_TILES], F32, name="pos_half")
-        nc.gpsimd.memset(pos_half[:], 0.5)
         warm_in = const.tile([P, 1], F32, name="warm_in")
         nc.vector.memset(warm_in[:], 0.0)
         warm_out = const.tile([P, 1], F32, name="warm_out")
@@ -70,29 +72,33 @@ def tile_layernormgrucell_pa_kernel(tc, x, h, W_irz, b_irz, W_hrz, b_hrz, out):
         ones = const.tile([P, P], BF16, name="ones")
         nc.vector.memset(ones[:], 1.0)
         bias_row = {}
-        for s in SIDES:
+        for s in (("x",) if BHDMA else SIDES):
             bias_row[s] = const.tile([P, G], BF16, name="bias_row_%s" % s)
             nc.vector.memset(bias_row[s][:].bitcast(U32), 0)
-        warm_rhs = const.tile([P, BANK], BF16, name="warm_rhs")
         if WARM:
-            nc.vector.memset(warm_rhs[:], 0.0)
+            warm_rhs = const.tile([P, BANK], BF16, name="warm_rhs")
+            nc.vector.memset(warm_rhs[:].bitcast(U32), 0)
 
         bias_bc = {}
         w_codes, w_scales, a_codes, a_scales = {}, {}, {}, {}
         bank_sum, neg_mean, sq_dev = {}, {}, {}
         for s in SIDES:
             bias_bc[s] = const.tile([P, G], BF16, name="bias_bc_%s" % s)
-            w_codes[s] = keep.tile([P, N_BLOCKS, PASSES * BANK], U32, name="w_codes_%s" % s, align_bytes=64)
-            w_scales[s] = keep.tile([P, N_BLOCKS, PASSES * BANK], U8, name="w_scales_%s" % s, align_bytes=64)
-            a_codes[s] = keep.tile([P, N_TILES, WORDS], U32, name="a_codes_%s" % s, align_bytes=64)
-            a_scales[s] = keep.tile([P, N_TILES, WORDS], U8, name="a_scales_%s" % s, align_bytes=64)
+            w_codes[s] = keep.tile([P, N_BLOCKS, PASSES * BANK], U32, name="w_codes_%s" % s, align_bytes=256)
+            w_scales[s] = keep.tile([P, N_BLOCKS, PASSES * BANK], U8, name="w_scales_%s" % s, align_bytes=256)
+            a_codes[s] = keep.tile([P, N_TILES, WORDS], U32, name="a_codes_%s" % s, align_bytes=256)
+            a_scales[s] = keep.tile([P, N_TILES, WORDS], U8, name="a_scales_%s" % s, align_bytes=256)
             bank_sum[s] = keep.tile([P, N_TILES, N_BLOCKS], F32, name="bank_sum_%s" % s)
             neg_mean[s] = keep.tile([P, N_TILES], F32, name="neg_mean_%s" % s)
             sq_dev[s] = keep.tile([P, N_TILES], F32, name="sq_dev_%s" % s)
         squares_out = keep.tile([P, G], BF16, name="squares_out")
+        var_eps = keep.tile([P, N_TILES], F32, name="var_eps")
         r_x = keep.tile([P, N_TILES], F32, name="r_x")
-        s_x = keep.tile([P, N_TILES], F32, name="s_x")
+        r2_x = keep.tile([P, N_TILES], F32, name="r2_x")
+        er_x = keep.tile([P, N_TILES], F32, name="er_x")
+        ms_x = keep.tile([P, N_TILES], F32, name="ms_x")
         nr_x = keep.tile([P, N_TILES], F32, name="nr_x")
+        rel = keep.tile([P, N_TILES], F32, name="rel")
         ratio = keep.tile([P, N_TILES], F32, name="ratio")
         shift = keep.tile([P, N_TILES], F32, name="shift")
 
@@ -101,16 +107,25 @@ def tile_layernormgrucell_pa_kernel(tc, x, h, W_irz, b_irz, W_hrz, b_hrz, out):
         grouped = {}
         acc = {}
         v = {}
+        spread = {}
 
         all_blocks = range(N_BLOCKS)
 
-        def load(key, rows):
-            raw[key] = raw_pool.tile([P, K], BF16, name="raw")
-            nc.sync.dma_start(out=raw[key][:], in_=rows)
+        def load(keys, rows):
+            n = len(keys)
+            if n == 1:
+                t = raw_pool.tile([P, K], BF16, name="raw1", bufs=4 if PAIRS else 20, align_bytes=256)
+                nc.sync.dma_start(out=t[:], in_=rows)
+                raw[keys[0]] = t[:]
+            else:
+                t2 = raw_pool.tile([P, n, K], BF16, name="raw2", bufs=9, align_bytes=256)
+                nc.sync.dma_start(out=t2[:], in_=rows.rearrange("(c p) k -> p c k", p=P))
+                for i in range(n):
+                    raw[keys[i]] = t2[:, i, :]
 
         def transpose(key):
-            turned[key] = tr_psum.tile([P, 2 * PASSES, P], F32, name="turned")
-            words = raw[key][:].bitcast(F32)
+            turned[key] = psum.tile([P, 2 * PASSES, P], F32, name="bank")
+            words = raw[key].bitcast(F32)
             for blk in range(2 * PASSES):
                 nc.tensor.transpose(turned[key][:, blk, :], words[:, blk * P:(blk + 1) * P], ident[:])
 
@@ -121,10 +136,8 @@ def tile_layernormgrucell_pa_kernel(tc, x, h, W_irz, b_irz, W_hrz, b_hrz, out):
             else:
                 nc.scalar.copy(out=dest, in_=src)
 
-        spread = {}
-
         def spread_matmul(s, half):
-            rep = spread[(s, half)] = tr_psum.tile([P, 2 * BANK], BF16, name="turned")
+            rep = spread[(s, half)] = psum.tile([P, 2 * BANK], BF16, name="bank")
             for i in range(2):
                 c0 = (2 * half + i) * BANK
                 nc.tensor.matmul(
@@ -141,7 +154,7 @@ def tile_layernormgrucell_pa_kernel(tc, x, h, W_irz, b_irz, W_hrz, b_hrz, out):
 
         def w_regroup(s, b, chunks, on_vector):
             if ("w", s, b) not in grouped:
-                grouped[("w", s, b)] = wq_pool.tile([P, 4 * PASSES * BANK], BF16, name="wq", align_bytes=64)
+                grouped[("w", s, b)] = wq_pool.tile([P, 4 * PASSES * BANK], BF16, name="wq", align_bytes=256)
             words = grouped[("w", s, b)][:].bitcast(F32).rearrange("q (g n u) -> q g n u", g=PASSES, n=BANK, u=2)
             for c in chunks:
                 regroup(("w", s, b, c), words[:, :, c * P:(c + 1) * P, :], on_vector)
@@ -154,11 +167,11 @@ def tile_layernormgrucell_pa_kernel(tc, x, h, W_irz, b_irz, W_hrz, b_hrz, out):
         def a_transpose(j):
             transpose(("a",) + JOBS[j])
 
-        def a_regroup(j):
+        def a_regroup(j, on_vector=False):
             key = ("a",) + JOBS[j]
-            grouped[key] = aq_pool.tile([P, 4 * WORDS], BF16, name="aq", align_bytes=64)
+            grouped[key] = aq_pool.tile([P, 4 * WORDS], BF16, name="aq", align_bytes=256)
             words = grouped[key][:].bitcast(F32).rearrange("q (g r u) -> q g r u", g=PASSES, r=P, u=2)
-            regroup(key, words, False)
+            regroup(key, words, on_vector)
 
         def a_quantise(j):
             s, t = JOBS[j]
@@ -169,7 +182,7 @@ def tile_layernormgrucell_pa_kernel(tc, x, h, W_irz, b_irz, W_hrz, b_hrz, out):
         def matmuls(j, blocks):
             s, t = JOBS[j]
             for b in blocks:
-                acc[(j, b)] = acc_psum.tile([P, BANK], F32, name="acc")
+                acc[(j, b)] = psum.tile([P, BANK], F32, name="bank")
                 for g in range(PASSES):
                     rows = slice(g * P, (g + 1) * P)
                     cols = slice(g * BANK, (g + 1) * BANK)
@@ -198,39 +211,47 @@ def tile_layernormgrucell_pa_kernel(tc, x, h, W_irz, b_irz, W_hrz, b_hrz, out):
             s, t = JOBS[j]
             scaled = tiny.tile([P, N_BLOCKS], F32, name="scaled")
             nc.scalar.activation(
-                out=scaled[:], in_=bank_sum[s][:, t, :], func=ACT.Identity, scale=-1.0 / G,
-                accum_out=neg_mean[s][:, t:t + 1],
+                out=scaled[:], in_=bank_sum[s][:, t, :], func=ACT.Identity,
+                scale=-1.0 / G if s == "x" else ms_x[:, t:t + 1], accum_out=neg_mean[s][:, t:t + 1],
             )
 
         def deviation(j):
             s, t = JOBS[j]
             one = slice(t, t + 1)
             nc.scalar.activation(
-                out=squares_out[:], in_=v[j][:], func=ACT.Square, bias=neg_mean[s][:, one], scale=1.0,
-                accum_out=sq_dev[s][:, one],
-            )
-            if s == "x":
-                return
-            var_eps = tiny.tile([P, 1], F32, name="var_eps")
-            nc.gpsimd.tensor_scalar(
-                out=var_eps[:], in0=sq_dev[s][:, one], scalar1=1.0 / G, scalar2=EPS, op0=ALU.mult, op1=ALU.add,
-            )
-            r_h = tiny.tile([P, 1], F32, name="r_h")
-            nc.gpsimd.tensor_tensor(out=r_h[:], in0=var_eps[:], in1=neg_half[:, 0:1], op=ALU.pow)
-            nc.gpsimd.tensor_tensor(out=ratio[:, one], in0=r_h[:], in1=s_x[:, one], op=ALU.mult)
-            nc.gpsimd.tensor_scalar(
-                out=shift[:, one], in0=r_h[:], scalar1=neg_mean[s][:, one], scalar2=nr_x[:, one],
-                op0=ALU.mult, op1=ALU.add,
+                out=squares_out[:], in_=v[j][:], func=ACT.Square, bias=neg_mean[s][:, one],
+                scale=1.0 if s == "x" else r_x[:, one], accum_out=sq_dev[s][:, one],
             )
 
-        def x_factors():
-            var_eps_x = keep.tile([P, N_TILES], F32, name="var_eps_x")
+        def x_factors(t0):
+            some = slice(t0, t0 + BATCH)
             nc.gpsimd.tensor_scalar(
-                out=var_eps_x[:], in0=sq_dev["x"][:], scalar1=1.0 / G, scalar2=EPS, op0=ALU.mult, op1=ALU.add,
+                out=var_eps[:, some], in0=sq_dev["x"][:, some], scalar1=1.0 / G, scalar2=EPS, op0=ALU.mult, op1=ALU.add,
             )
-            nc.gpsimd.tensor_tensor(out=r_x[:], in0=var_eps_x[:], in1=neg_half[:], op=ALU.pow)
-            nc.gpsimd.tensor_tensor(out=s_x[:], in0=var_eps_x[:], in1=pos_half[:], op=ALU.pow)
-            nc.gpsimd.tensor_tensor(out=nr_x[:], in0=neg_mean["x"][:], in1=r_x[:], op=ALU.mult)
+            nc.gpsimd.tensor_tensor(out=r_x[:, some], in0=var_eps[:, some], in1=neg_half[:, some], op=ALU.pow)
+            nc.gpsimd.tensor_scalar(
+                out=ms_x[:, some], in0=r_x[:, some], scalar1=-1.0 / G, scalar2=0.0, op0=ALU.mult, op1=ALU.add,
+            )
+            nc.gpsimd.tensor_tensor(out=nr_x[:, some], in0=neg_mean["x"][:, some], in1=r_x[:, some], op=ALU.mult)
+            nc.gpsimd.tensor_tensor(out=r2_x[:, some], in0=r_x[:, some], in1=r_x[:, some], op=ALU.mult)
+            nc.gpsimd.tensor_scalar(
+                out=er_x[:, some], in0=r2_x[:, some], scalar1=EPS, scalar2=0.0, op0=ALU.mult, op1=ALU.add,
+            )
+
+        def relation(j):
+            t = JOBS[j][1]
+            one = slice(t, t + 1)
+            nc.scalar.activation(
+                out=rel[:, one], in_=sq_dev["h"][:, one], func=ACT.Identity, scale=1.0 / G, bias=er_x[:, one],
+            )
+            nc.gpsimd.tensor_tensor(out=ratio[:, one], in0=rel[:, one], in1=neg_half[:, 0:1], op=ALU.pow)
+
+        def shifts(j):
+            t = JOBS[j][1]
+            one = slice(t, t + 1)
+            nc.scalar.activation(
+                out=shift[:, one], in_=neg_mean["h"][:, one], func=ACT.Identity, scale=ratio[:, one], bias=nr_x[:, one],
+            )
 
         def combine(j):
             t = JOBS[j][1]
@@ -259,20 +280,23 @@ def tile_layernormgrucell_pa_kernel(tc, x, h, W_irz, b_irz, W_hrz, b_hrz, out):
         with tc.manual_schedule():
             for s in SIDES:
                 for b in all_blocks:
-                    for c in range(4):
+                    step = 1 if (b == 0 and s == "x") or not PAIRS else 2
+                    for c in range(0, 4, step):
                         r0 = b * BANK + c * P
-                        load(("w", s, b, c), wgt_dram[s][r0:r0 + P, :])
+                        load([("w", s, b, c + i) for i in range(step)], wgt_dram[s][r0:r0 + step * P, :])
                     if b == 0:
                         if s == "x":
-                            nc.sync.dma_start(out=bias_row["x"][0:1, :], in_=b_irz.unsqueeze(0))
-                            nc.sync.dma_start(out=bias_row["h"][0:1, :], in_=b_hrz.unsqueeze(0))
-                        for t in range(EARLY):
-                            load(("a", s, t), act_dram[s][t * P:(t + 1) * P, :])
-                for t in range(EARLY, N_TILES):
-                    load(("a", s, t), act_dram[s][t * P:(t + 1) * P, :])
+                            for s2 in bias_row:
+                                nc.sync.dma_start(out=bias_row[s2][0:1, :], in_=(b_irz if s2 == "x" else b_hrz).unsqueeze(0))
+                    step = 2 if PAIRS else 1
+                    for t in range(0, EARLY if b == 0 else N_TILES if b == N_BLOCKS - 1 else 0, step):
+                        if b == 0 or t >= EARLY:
+                            load([("a", s, t + i) for i in range(step)], act_dram[s][t * P:(t + step) * P, :])
+            if BHDMA:
+                nc.sync.dma_start(out=bias_bc["h"][:], in_=b_hrz.partition_broadcast(P))
 
             for i in range(WARM):
-                warm_bank = tr_psum.tile([P, BANK], F32, name="turned")
+                warm_bank = psum.tile([P, BANK], F32, name="bank")
                 nc.tensor.matmul(out=warm_bank[:], lhsT=ones[:], rhs=warm_rhs[:], start=True, stop=True)
             for b in range(N_BLOCKS + 1):
                 if b < N_BLOCKS:
@@ -300,7 +324,7 @@ def tile_layernormgrucell_pa_kernel(tc, x, h, W_irz, b_irz, W_hrz, b_hrz, out):
             matmuls(EARLY, all_blocks)
             for j in range(EARLY):
                 mean(j)
-                if j < EARLY - DL:
+                if j < EARLY - 1:
                     deviation(j)
             for n in range(EARLY, N_JOBS + GL):
                 b = n - EARLY
@@ -308,7 +332,7 @@ def tile_layernormgrucell_pa_kernel(tc, x, h, W_irz, b_irz, W_hrz, b_hrz, out):
                     a_transpose(n + 3)
                 if b < N_BLOCKS:
                     w_transpose("h", b)
-                if HS <= n < HS + 2:
+                if not BHDMA and HS <= n < HS + 2:
                     spread_matmul("h", n - HS)
                 if is_job(n + 1):
                     matmuls(n + 1, all_blocks)
@@ -321,17 +345,24 @@ def tile_layernormgrucell_pa_kernel(tc, x, h, W_irz, b_irz, W_hrz, b_hrz, out):
                         combine(n - CL)
                     if o == "a" and is_job(n + 2, EARLY + 2):
                         a_quantise(n + 2)
+                    if o == "r" and n + 3 in AV:
+                        a_regroup(n + 3, True)
                     if o == "v":
                         if b < N_BLOCKS:
                             w_regroup("h", b, HV[b], True)
-                        if HS <= n < HS + 2:
+                        if not BHDMA and HS <= n < HS + 2:
                             spread_copy("h", n - HS)
                 for o in (SX if n < N_TILES else SH):
-                    if o == "d" and is_job(n - DL):
-                        deviation(n - DL)
-                    if o == "f" and n == N_TILES + DL - 1:
-                        x_factors()
-                    if o == "a" and is_job(n + 3, EARLY + 3):
+                    if o == "d" and is_job(n - 1):
+                        deviation(n - 1)
+                        if n <= N_TILES and n % BATCH == 0:
+                            x_factors(n - BATCH)
+                    if o == "t":
+                        if is_job(n - 1, N_TILES):
+                            relation(n - 1)
+                        if is_job(n - 2, N_TILES):
+                            shifts(n - 2)
+                    if o == "a" and is_job(n + 3, EARLY + 3) and n + 3 not in AV:
                         a_regroup(n + 3)
                     if o == "m" and is_job(n):
                         mean(n)

@@ -241,16 +241,17 @@ def tile_layernormgrucell_pa_kernel(tc, x, h, W_irz, b_irz, W_hrz, b_hrz, out):
         def relation(j):
             t = JOBS[j][1]
             one = slice(t, t + 1)
-            nc.scalar.activation(
-                out=rel[:, one], in_=sq_dev["h"][:, one], func=ACT.Identity, scale=1.0 / G, bias=er_x[:, one],
+            nc.gpsimd.tensor_scalar(
+                out=rel[:, one], in0=sq_dev["h"][:, one], scalar1=1.0 / G, scalar2=er_x[:, one], op0=ALU.mult, op1=ALU.add,
             )
             nc.gpsimd.tensor_tensor(out=ratio[:, one], in0=rel[:, one], in1=neg_half[:, 0:1], op=ALU.pow)
 
         def shifts(j):
             t = JOBS[j][1]
             one = slice(t, t + 1)
-            nc.scalar.activation(
-                out=shift[:, one], in_=neg_mean["h"][:, one], func=ACT.Identity, scale=ratio[:, one], bias=nr_x[:, one],
+            nc.gpsimd.tensor_scalar(
+                out=shift[:, one], in0=neg_mean["h"][:, one], scalar1=ratio[:, one], scalar2=nr_x[:, one],
+                op0=ALU.mult, op1=ALU.add,
             )
 
         def combine(j):
@@ -360,8 +361,7 @@ def tile_layernormgrucell_pa_kernel(tc, x, h, W_irz, b_irz, W_hrz, b_hrz, out):
                     if o == "t":
                         if is_job(n - 1, N_TILES):
                             relation(n - 1)
-                        if is_job(n - 2, N_TILES):
-                            shifts(n - 2)
+                            shifts(n - 1)
                     if o == "a" and is_job(n + 3, EARLY + 3) and n + 3 not in AV:
                         a_regroup(n + 3)
                     if o == "m" and is_job(n):

@@ -36,13 +36,16 @@ HV = ((3,), (3,), (3,), (3,))
 XV = ((), (), (), ())
 VX = "eaqv"
 VH = "erac"
-SX = "awdm"
-SH = "dgmat"
+SX = "mdawf"
+SH = "dgmatf"
 CL, GL = 2, 3
 TQ = 2
 HALVES = 2
 BATCH = 4
-AV = (13, 15)
+QAT = 1
+QP = 2
+X_STAGES = (("pair_a", "pair_b", "var_c", "total", "minus_mean"), ("off", "off2"), ())
+AV = ()
 
 
 def tile_layernormgrucell_pa_kernel(tc, x, h, W_irz, b_irz, W_hrz, b_hrz, out):
@@ -108,6 +111,7 @@ def tile_layernormgrucell_pa_kernel(tc, x, h, W_irz, b_irz, W_hrz, b_hrz, out):
         acc = {}
         v = {}
         spread = {}
+        x_temps = {}
 
         all_blocks = range(N_BLOCKS)
 
@@ -160,9 +164,14 @@ def tile_layernormgrucell_pa_kernel(tc, x, h, W_irz, b_irz, W_hrz, b_hrz, out):
                 regroup(("w", s, b, c), words[:, :, c * P:(c + 1) * P, :], on_vector)
 
         def w_quantise(s, b):
-            nc.vector.quantize_mx(
-                out=w_codes[s][:, b, :].bitcast(FP8X4), scales=w_scales[s][:, b, :], in_=grouped[("w", s, b)][:],
-            )
+            parts = QP if s == "x" else 1
+            n = PASSES * BANK // parts
+            for i in range(parts):
+                span = slice(i * n, (i + 1) * n)
+                nc.vector.quantize_mx(
+                    out=w_codes[s][:, b, span].bitcast(FP8X4), scales=w_scales[s][:, b, span],
+                    in_=grouped[("w", s, b)][:, i * 4 * n:(i + 1) * 4 * n],
+                )
 
         def a_transpose(j):
             transpose(("a",) + JOBS[j])
@@ -207,12 +216,22 @@ def tile_layernormgrucell_pa_kernel(tc, x, h, W_irz, b_irz, W_hrz, b_hrz, out):
                     op0=ALU.mult, op1=ALU.add, accum_out=bank_sum[s][:, t, b:b + 1],
                 )
 
+        def center(j):
+            t = JOBS[j][1]
+            nc.gpsimd.tensor_scalar(
+                out=neg_mean["x"][:, t:t + 1], in0=bank_sum["x"][:, t, 0:1], scalar1=-1.0 / BANK, scalar2=0.0,
+                op0=ALU.mult, op1=ALU.add,
+            )
+
         def mean(j):
             s, t = JOBS[j]
+            if s == "x":
+                center(j)
+                return
             scaled = tiny.tile([P, N_BLOCKS], F32, name="scaled")
             nc.scalar.activation(
                 out=scaled[:], in_=bank_sum[s][:, t, :], func=ACT.Identity,
-                scale=-1.0 / G if s == "x" else ms_x[:, t:t + 1], accum_out=neg_mean[s][:, t:t + 1],
+                scale=ms_x[:, t:t + 1], accum_out=neg_mean[s][:, t:t + 1],
             )
 
         def deviation(j):
@@ -223,20 +242,36 @@ def tile_layernormgrucell_pa_kernel(tc, x, h, W_irz, b_irz, W_hrz, b_hrz, out):
                 scale=1.0 if s == "x" else r_x[:, one], accum_out=sq_dev[s][:, one],
             )
 
-        def x_factors(t0):
+        def x_factors(t0, stage):
             some = slice(t0, t0 + BATCH)
-            nc.gpsimd.tensor_scalar(
-                out=var_eps[:, some], in0=sq_dev["x"][:, some], scalar1=1.0 / G, scalar2=EPS, op0=ALU.mult, op1=ALU.add,
-            )
-            nc.gpsimd.tensor_tensor(out=r_x[:, some], in0=var_eps[:, some], in1=neg_half[:, some], op=ALU.pow)
-            nc.gpsimd.tensor_scalar(
-                out=ms_x[:, some], in0=r_x[:, some], scalar1=-1.0 / G, scalar2=0.0, op0=ALU.mult, op1=ALU.add,
-            )
-            nc.gpsimd.tensor_tensor(out=nr_x[:, some], in0=neg_mean["x"][:, some], in1=r_x[:, some], op=ALU.mult)
-            nc.gpsimd.tensor_tensor(out=r2_x[:, some], in0=r_x[:, some], in1=r_x[:, some], op=ALU.mult)
-            nc.gpsimd.tensor_scalar(
-                out=er_x[:, some], in0=r2_x[:, some], scalar1=EPS, scalar2=0.0, op0=ALU.mult, op1=ALU.add,
-            )
+            sums = bank_sum["x"]
+            tmp = x_temps.setdefault(t0, {})
+            for nm in X_STAGES[stage]:
+                tmp[nm] = tiny.tile([P, BATCH], F32, name=nm)
+            if stage == 0:
+                nc.gpsimd.tensor_tensor(out=tmp["pair_a"][:], in0=sums[:, some, 0], in1=sums[:, some, 1], op=ALU.add)
+                nc.gpsimd.tensor_tensor(out=tmp["pair_b"][:], in0=sums[:, some, 2], in1=sums[:, some, 3], op=ALU.add)
+                nc.gpsimd.tensor_scalar(
+                    out=tmp["var_c"][:], in0=sq_dev["x"][:, some], scalar1=1.0 / G, scalar2=EPS, op0=ALU.mult, op1=ALU.add,
+                )
+                nc.gpsimd.tensor_tensor(out=tmp["total"][:], in0=tmp["pair_a"][:], in1=tmp["pair_b"][:], op=ALU.add)
+                nc.gpsimd.tensor_scalar(
+                    out=tmp["minus_mean"][:], in0=tmp["total"][:], scalar1=-1.0 / G, scalar2=0.0, op0=ALU.mult, op1=ALU.add,
+                )
+            if stage == 1:
+                nc.gpsimd.tensor_tensor(out=tmp["off"][:], in0=tmp["minus_mean"][:], in1=neg_mean["x"][:, some], op=ALU.subtract)
+                nc.gpsimd.tensor_tensor(out=tmp["off2"][:], in0=tmp["off"][:], in1=tmp["off"][:], op=ALU.mult)
+                nc.gpsimd.tensor_tensor(out=var_eps[:, some], in0=tmp["var_c"][:], in1=tmp["off2"][:], op=ALU.subtract)
+            if stage == 2:
+                nc.gpsimd.tensor_tensor(out=r_x[:, some], in0=var_eps[:, some], in1=neg_half[:, some], op=ALU.pow)
+                nc.gpsimd.tensor_scalar(
+                    out=ms_x[:, some], in0=r_x[:, some], scalar1=-1.0 / G, scalar2=0.0, op0=ALU.mult, op1=ALU.add,
+                )
+                nc.gpsimd.tensor_tensor(out=nr_x[:, some], in0=tmp["minus_mean"][:], in1=r_x[:, some], op=ALU.mult)
+                nc.gpsimd.tensor_tensor(out=r2_x[:, some], in0=r_x[:, some], in1=r_x[:, some], op=ALU.mult)
+                nc.gpsimd.tensor_scalar(
+                    out=er_x[:, some], in0=r2_x[:, some], scalar1=EPS, scalar2=0.0, op0=ALU.mult, op1=ALU.add,
+                )
 
         def relation(j):
             t = JOBS[j][1]
@@ -307,7 +342,8 @@ def tile_layernormgrucell_pa_kernel(tc, x, h, W_irz, b_irz, W_hrz, b_hrz, out):
                     if b < 2:
                         spread_matmul("x", b)
                         spread_copy("x", b)
-                    w_quantise("x", b)
+                    if b == 0:
+                        w_quantise("x", b)
                 for j in range(EARLY):
                     if b == 0:
                         a_transpose(j)
@@ -315,7 +351,12 @@ def tile_layernormgrucell_pa_kernel(tc, x, h, W_irz, b_irz, W_hrz, b_hrz, out):
                         a_quantise(j)
                     else:
                         matmuls(j, [b - 1])
+                        if j == QAT:
+                            if b < N_BLOCKS:
+                                w_quantise("x", b)
                         bias_add(j, [b - 1])
+                if QAT == 2 and 0 < b < N_BLOCKS:
+                    w_quantise("x", b)
                 if b == N_BLOCKS - 1:
                     for j in range(EARLY, EARLY + 3):
                         a_transpose(j)
@@ -356,8 +397,8 @@ def tile_layernormgrucell_pa_kernel(tc, x, h, W_irz, b_irz, W_hrz, b_hrz, out):
                 for o in (SX if n < N_TILES else SH):
                     if o == "d" and is_job(n - 1):
                         deviation(n - 1)
-                        if n <= N_TILES and n % BATCH == 0:
-                            x_factors(n - BATCH)
+                    if o == "f" and BATCH <= n < BATCH + N_TILES and n % BATCH < len(X_STAGES):
+                        x_factors((n // BATCH - 1) * BATCH, n % BATCH)
                     if o == "t":
                         if is_job(n - 1, N_TILES):
                             relation(n - 1)

@@ -27,7 +27,7 @@ SIDES = ("x", "h")
 JOBS = tuple((side, t) for side in SIDES for t in range(N_TILES))
 N_JOBS = len(JOBS)
 EARLY = 2
-WARM = 0
+WARM = 4
 PAIRS = 0
 SG = 1
 BHDMA = 1
@@ -339,9 +339,6 @@ def tile_layernormgrucell_pa_kernel(tc, x, h, W_irz, b_irz, W_hrz, b_hrz, out):
                     w_transpose("x", b)
                     w_regroup("x", b, [c for c in range(4) if c not in XV[b]], False)
                     w_regroup("x", b, XV[b], True)
-                    if b < 2:
-                        spread_matmul("x", b)
-                        spread_copy("x", b)
                     if b == 0:
                         w_quantise("x", b)
                 for j in range(EARLY):
@@ -349,6 +346,8 @@ def tile_layernormgrucell_pa_kernel(tc, x, h, W_irz, b_irz, W_hrz, b_hrz, out):
                         a_transpose(j)
                         a_regroup(j)
                         a_quantise(j)
+                        spread_matmul("x", j)
+                        spread_copy("x", j)
                     else:
                         matmuls(j, [b - 1])
                         if j == QAT:

from contextlib import ExitStack

import concourse.mybir as mybir
from concourse.masks import make_identity

F32 = mybir.dt.float32
BF16 = mybir.dt.bfloat16
U32 = mybir.dt.uint32
U8 = mybir.dt.uint8
FP8X4 = mybir.dt.float8_e4m3fn_x4
ALU = mybir.AluOpType
ACT = mybir.ActivationFunctionType

P = 128
B = 1024
K = 1024
G = 2048
EPS = 1e-5
BANK = 512
PASSES = K // 512
N_TILES = B // P
N_BLOCKS = G // BANK
WORDS = PASSES * P
FLOPS = 2 * 2 * B * K * G

SIDES = ("x", "h")
JOBS = tuple((side, t) for side in SIDES for t in range(N_TILES))
N_JOBS = len(JOBS)
EARLY = 2
WARM = 4
PAIRS = 0
SG = 1
BHDMA = 1
HS = 6
HV = ((3,), (3,), (3,), (3,))
XV = ((), (), (), ())
VX = "eaqv"
VH = "erac"
SX = "mdawf"
SH = "dgmatf"
CL, GL = 2, 3
TQ = 2
HALVES = 2
BATCH = 4
QAT = 1
QP = 2
X_STAGES = (("pair_a", "pair_b", "var_c", "total", "minus_mean"), ("off", "off2"), ())
AV = ()


def tile_layernormgrucell_pa_kernel(tc, x, h, W_irz, b_irz, W_hrz, b_hrz, out):
    nc = tc.nc
    act_dram = {"x": x, "h": h}
    wgt_dram = {"x": W_irz, "h": W_hrz}

    with ExitStack() as ctx:
        const = ctx.enter_context(tc.tile_pool(name="const", bufs=1))
        keep = ctx.enter_context(tc.tile_pool(name="keep", bufs=1))
        raw_pool = ctx.enter_context(tc.tile_pool(name="raw_pool", bufs=6))
        wq_pool = ctx.enter_context(tc.tile_pool(name="wq_pool", bufs=2))
        aq_pool = ctx.enter_context(tc.tile_pool(name="aq_pool", bufs=4))
        v_pool = ctx.enter_context(tc.tile_pool(name="v_pool", bufs=N_TILES + 3))
        tiny = ctx.enter_context(tc.tile_pool(name="tiny", bufs=4))
        psum = ctx.enter_context(tc.psum_pool(name="psum", bufs=8))

        ident = const.tile([P, P], F32, name="ident")
        make_identity(nc, ident[:])
        neg_half = const.tile([P, N_TILES], F32, name="neg_half")
        nc.gpsimd.memset(neg_half[:], -0.5)
        warm_in = const.tile([P, 1], F32, name="warm_in")
        nc.vector.memset(warm_in[:], 0.0)
        warm_out = const.tile([P, 1], F32, name="warm_out")
        nc.scalar.activation(out=warm_out[:], in_=warm_in[:], func=ACT.Sigmoid)

        ones = const.tile([P, P], BF16, name="ones")
        nc.vector.memset(ones[:], 1.0)
        bias_row = {}
        for s in (("x",) if BHDMA else SIDES):
            bias_row[s] = const.tile([P, G], BF16, name="bias_row_%s" % s)
            nc.vector.memset(bias_row[s][:].bitcast(U32), 0)
        if WARM:
            warm_rhs = const.tile([P, BANK], BF16, name="warm_rhs")
            nc.vector.memset(warm_rhs[:].bitcast(U32), 0)

        bias_bc = {}
        w_codes, w_scales, a_codes, a_scales = {}, {}, {}, {}
        bank_sum, neg_mean, sq_dev = {}, {}, {}
        for s in SIDES:
            bias_bc[s] = const.tile([P, G], BF16, name="bias_bc_%s" % s)
            w_codes[s] = keep.tile([P, N_BLOCKS, PASSES * BANK], U32, name="w_codes_%s" % s, align_bytes=256)
            w_scales[s] = keep.tile([P, N_BLOCKS, PASSES * BANK], U8, name="w_scales_%s" % s, align_bytes=256)
            a_codes[s] = keep.tile([P, N_TILES, WORDS], U32, name="a_codes_%s" % s, align_bytes=256)
            a_scales[s] = keep.tile([P, N_TILES, WORDS], U8, name="a_scales_%s" % s, align_bytes=256)
            bank_sum[s] = keep.tile([P, N_TILES, N_BLOCKS], F32, name="bank_sum_%s" % s)
            neg_mean[s] = keep.tile([P, N_TILES], F32, name="neg_mean_%s" % s)
            sq_dev[s] = keep.tile([P, N_TILES], F32, name="sq_dev_%s" % s)
        squares_out = keep.tile([P, G], BF16, name="squares_out")
        var_eps = keep.tile([P, N_TILES], F32, name="var_eps")
        r_x = keep.tile([P, N_TILES], F32, name="r_x")
        r2_x = keep.tile([P, N_TILES], F32, name="r2_x")
        er_x = keep.tile([P, N_TILES], F32, name="er_x")
        ms_x = keep.tile([P, N_TILES], F32, name="ms_x")
        nr_x = keep.tile([P, N_TILES], F32, name="nr_x")
        rel = keep.tile([P, N_TILES], F32, name="rel")
        ratio = keep.tile([P, N_TILES], F32, name="ratio")
        shift = keep.tile([P, N_TILES], F32, name="shift")

        raw = {}
        turned = {}
        grouped = {}
        acc = {}
        v = {}
        spread = {}
        x_temps = {}

        all_blocks = range(N_BLOCKS)

        def load(keys, rows):
            n = len(keys)
            if n == 1:
                t = raw_pool.tile([P, K], BF16, name="raw1", bufs=4 if PAIRS else 20, align_bytes=256)
                nc.sync.dma_start(out=t[:], in_=rows)
                raw[keys[0]] = t[:]
            else:
                t2 = raw_pool.tile([P, n, K], BF16, name="raw2", bufs=9, align_bytes=256)
                nc.sync.dma_start(out=t2[:], in_=rows.rearrange("(c p) k -> p c k", p=P))
                for i in range(n):
                    raw[keys[i]] = t2[:, i, :]

        def transpose(key):
            turned[key] = psum.tile([P, 2 * PASSES, P], F32, name="bank")
            words = raw[key].bitcast(F32)
            for blk in range(2 * PASSES):
                nc.tensor.transpose(turned[key][:, blk, :], words[:, blk * P:(blk + 1) * P], ident[:])

        def regroup(key, dest, on_vector):
            src = turned[key][:].rearrange("q (g u) r -> q g r u", g=PASSES, u=2)
            if on_vector:
                nc.vector.tensor_copy(out=dest, in_=src)
            else:
                nc.scalar.copy(out=dest, in_=src)

        def spread_matmul(s, half):
            rep = spread[(s, half)] = psum.tile([P, 2 * BANK], BF16, name="bank")
            for i in range(2):
                c0 = (2 * half + i) * BANK
                nc.tensor.matmul(
                    out=rep[:, i * BANK:(i + 1) * BANK], lhsT=ones[:], rhs=bias_row[s][:, c0:c0 + BANK],
                    start=True, stop=True,
                )

        def spread_copy(s, half):
            nc.vector.tensor_copy(out=bias_bc[s][:, 2 * half * BANK:(2 * half + 2) * BANK], in_=spread[(s, half)][:])

        def w_transpose(s, b):
            for c in range(4):
                transpose(("w", s, b, c))

        def w_regroup(s, b, chunks, on_vector):
            if ("w", s, b) not in grouped:
                grouped[("w", s, b)] = wq_pool.tile([P, 4 * PASSES * BANK], BF16, name="wq", align_bytes=256)
            words = grouped[("w", s, b)][:].bitcast(F32).rearrange("q (g n u) -> q g n u", g=PASSES, n=BANK, u=2)
            for c in chunks:
                regroup(("w", s, b, c), words[:, :, c * P:(c + 1) * P, :], on_vector)

        def w_quantise(s, b):
            parts = QP if s == "x" else 1
            n = PASSES * BANK // parts
            for i in range(parts):
                span = slice(i * n, (i + 1) * n)
                nc.vector.quantize_mx(
                    out=w_codes[s][:, b, span].bitcast(FP8X4), scales=w_scales[s][:, b, span],
                    in_=grouped[("w", s, b)][:, i * 4 * n:(i + 1) * 4 * n],
                )

        def a_transpose(j):
            transpose(("a",) + JOBS[j])

        def a_regroup(j, on_vector=False):
            key = ("a",) + JOBS[j]
            grouped[key] = aq_pool.tile([P, 4 * WORDS], BF16, name="aq", align_bytes=256)
            words = grouped[key][:].bitcast(F32).rearrange("q (g r u) -> q g r u", g=PASSES, r=P, u=2)
            regroup(key, words, on_vector)

        def a_quantise(j):
            s, t = JOBS[j]
            nc.vector.quantize_mx(
                out=a_codes[s][:, t, :].bitcast(FP8X4), scales=a_scales[s][:, t, :], in_=grouped[("a", s, t)][:],
            )

        def matmuls(j, blocks):
            s, t = JOBS[j]
            for b in blocks:
                acc[(j, b)] = psum.tile([P, BANK], F32, name="bank")
                for g in range(PASSES):
                    rows = slice(g * P, (g + 1) * P)
                    cols = slice(g * BANK, (g + 1) * BANK)
                    nc.tensor.matmul_mx(
                        out=acc[(j, b)][:],
                        lhsT=a_codes[s][:, t, rows].bitcast(FP8X4),
                        lhsT_scale=a_scales[s][:, t, rows],
                        rhs=w_codes[s][:, b, cols].bitcast(FP8X4),
                        rhs_scale=w_scales[s][:, b, cols],
                        start=(g == 0),
                        stop=(g == PASSES - 1),
                    )

        def bias_add(j, blocks):
            s, t = JOBS[j]
            if j not in v:
                v[j] = v_pool.tile([P, G], F32, name="v")
            for b in blocks:
                cols = slice(b * BANK, (b + 1) * BANK)
                nc.vector.scalar_tensor_tensor(
                    out=v[j][:, cols], in0=acc[(j, b)][:], scalar=1.0, in1=bias_bc[s][:, cols],
                    op0=ALU.mult, op1=ALU.add, accum_out=bank_sum[s][:, t, b:b + 1],
                )

        def center(j):
            t = JOBS[j][1]
            nc.gpsimd.tensor_scalar(
                out=neg_mean["x"][:, t:t + 1], in0=bank_sum["x"][:, t, 0:1], scalar1=-1.0 / BANK, scalar2=0.0,
                op0=ALU.mult, op1=ALU.add,
            )

        def mean(j):
            s, t = JOBS[j]
            if s == "x":
                center(j)
                return
            scaled = tiny.tile([P, N_BLOCKS], F32, name="scaled")
            nc.scalar.activation(
                out=scaled[:], in_=bank_sum[s][:, t, :], func=ACT.Identity,
                scale=ms_x[:, t:t + 1], accum_out=neg_mean[s][:, t:t + 1],
            )

        def deviation(j):
            s, t = JOBS[j]
            one = slice(t, t + 1)
            nc.scalar.activation(
                out=squares_out[:], in_=v[j][:], func=ACT.Square, bias=neg_mean[s][:, one],
                scale=1.0 if s == "x" else r_x[:, one], accum_out=sq_dev[s][:, one],
            )

        def x_factors(t0, stage):
            some = slice(t0, t0 + BATCH)
            sums = bank_sum["x"]
            tmp = x_temps.setdefault(t0, {})
            for nm in X_STAGES[stage]:
                tmp[nm] = tiny.tile([P, BATCH], F32, name=nm)
            if stage == 0:
                nc.gpsimd.tensor_tensor(out=tmp["pair_a"][:], in0=sums[:, some, 0], in1=sums[:, some, 1], op=ALU.add)
                nc.gpsimd.tensor_tensor(out=tmp["pair_b"][:], in0=sums[:, some, 2], in1=sums[:, some, 3], op=ALU.add)
                nc.gpsimd.tensor_scalar(
                    out=tmp["var_c"][:], in0=sq_dev["x"][:, some], scalar1=1.0 / G, scalar2=EPS, op0=ALU.mult, op1=ALU.add,
                )
                nc.gpsimd.tensor_tensor(out=tmp["total"][:], in0=tmp["pair_a"][:], in1=tmp["pair_b"][:], op=ALU.add)
                nc.gpsimd.tensor_scalar(
                    out=tmp["minus_mean"][:], in0=tmp["total"][:], scalar1=-1.0 / G, scalar2=0.0, op0=ALU.mult, op1=ALU.add,
                )
            if stage == 1:
                nc.gpsimd.tensor_tensor(out=tmp["off"][:], in0=tmp["minus_mean"][:], in1=neg_mean["x"][:, some], op=ALU.subtract)
                nc.gpsimd.tensor_tensor(out=tmp["off2"][:], in0=tmp["off"][:], in1=tmp["off"][:], op=ALU.mult)
                nc.gpsimd.tensor_tensor(out=var_eps[:, some], in0=tmp["var_c"][:], in1=tmp["off2"][:], op=ALU.subtract)
            if stage == 2:
                nc.gpsimd.tensor_tensor(out=r_x[:, some], in0=var_eps[:, some], in1=neg_half[:, some], op=ALU.pow)
                nc.gpsimd.tensor_scalar(
                    out=ms_x[:, some], in0=r_x[:, some], scalar1=-1.0 / G, scalar2=0.0, op0=ALU.mult, op1=ALU.add,
                )
                nc.gpsimd.tensor_tensor(out=nr_x[:, some], in0=tmp["minus_mean"][:], in1=r_x[:, some], op=ALU.mult)
                nc.gpsimd.tensor_tensor(out=r2_x[:, some], in0=r_x[:, some], in1=r_x[:, some], op=ALU.mult)
                nc.gpsimd.tensor_scalar(
                    out=er_x[:, some], in0=r2_x[:, some], scalar1=EPS, scalar2=0.0, op0=ALU.mult, op1=ALU.add,
                )

        def relation(j):
            t = JOBS[j][1]
            one = slice(t, t + 1)
            nc.gpsimd.tensor_scalar(
                out=rel[:, one], in0=sq_dev["h"][:, one], scalar1=1.0 / G, scalar2=er_x[:, one], op0=ALU.mult, op1=ALU.add,
            )
            nc.gpsimd.tensor_tensor(out=ratio[:, one], in0=rel[:, one], in1=neg_half[:, 0:1], op=ALU.pow)

        def shifts(j):
            t = JOBS[j][1]
            one = slice(t, t + 1)
            nc.gpsimd.tensor_scalar(
                out=shift[:, one], in0=neg_mean["h"][:, one], scalar1=ratio[:, one], scalar2=nr_x[:, one],
                op0=ALU.mult, op1=ALU.add,
            )

        def combine(j):
            t = JOBS[j][1]
            n_pieces = TQ if j == N_JOBS - 1 else 1
            for i in range(n_pieces):
                cols = slice(i * G // n_pieces, (i + 1) * G // n_pieces)
                nc.vector.scalar_tensor_tensor(
                    out=v[j][:, cols], in0=v[j][:, cols], scalar=ratio[:, t:t + 1], in1=v[t][:, cols],
                    op0=ALU.mult, op1=ALU.add,
                )

        def gate(j):
            t = JOBS[j][1]
            n_pieces = TQ if j == N_JOBS - 1 else HALVES
            for i in range(n_pieces):
                cols = slice(i * G // n_pieces, (i + 1) * G // n_pieces)
                nc.scalar.activation(
                    out=v[j][:, cols], in_=v[j][:, cols], func=ACT.Sigmoid,
                    bias=shift[:, t:t + 1], scale=r_x[:, t:t + 1],
                )
                nc.sync.dma_start(out=out[t * P:(t + 1) * P, cols], in_=v[j][:, cols])

        def is_job(j, first=0):
            return first <= j < N_JOBS

        with tc.manual_schedule():
            for s in SIDES:
                for b in all_blocks:
                    step = 1 if (b == 0 and s == "x") or not PAIRS else 2
                    for c in range(0, 4, step):
                        r0 = b * BANK + c * P
                        load([("w", s, b, c + i) for i in range(step)], wgt_dram[s][r0:r0 + step * P, :])
                    if b == 0:
                        if s == "x":
                            for s2 in bias_row:
                                nc.sync.dma_start(out=bias_row[s2][0:1, :], in_=(b_irz if s2 == "x" else b_hrz).unsqueeze(0))
                    step = 2 if PAIRS else 1
                    for t in range(0, EARLY if b == 0 else N_TILES if b == N_BLOCKS - 1 else 0, step):
                        if b == 0 or t >= EARLY:
                            load([("a", s, t + i) for i in range(step)], act_dram[s][t * P:(t + step) * P, :])
            if BHDMA:
                nc.sync.dma_start(out=bias_bc["h"][:], in_=b_hrz.partition_broadcast(P))

            for i in range(WARM):
                warm_bank = psum.tile([P, BANK], F32, name="bank")
                nc.tensor.matmul(out=warm_bank[:], lhsT=ones[:], rhs=warm_rhs[:], start=True, stop=True)
            for b in range(N_BLOCKS + 1):
                if b < N_BLOCKS:
                    w_transpose("x", b)
                    w_regroup("x", b, [c for c in range(4) if c not in XV[b]], False)
                    w_regroup("x", b, XV[b], True)
                    if b == 0:
                        w_quantise("x", b)
                for j in range(EARLY):
                    if b == 0:
                        a_transpose(j)
                        a_regroup(j)
                        a_quantise(j)
                        spread_matmul("x", j)
                        spread_copy("x", j)
                    else:
                        matmuls(j, [b - 1])
                        if j == QAT:
                            if b < N_BLOCKS:
                                w_quantise("x", b)
                        bias_add(j, [b - 1])
                if QAT == 2 and 0 < b < N_BLOCKS:
                    w_quantise("x", b)
                if b == N_BLOCKS - 1:
                    for j in range(EARLY, EARLY + 3):
                        a_transpose(j)
                        a_regroup(j)
                    for j in range(EARLY, EARLY + 2):
                        a_quantise(j)
            matmuls(EARLY, all_blocks)
            for j in range(EARLY):
                mean(j)
                if j < EARLY - 1:
                    deviation(j)
            for n in range(EARLY, N_JOBS + GL):
                b = n - EARLY
                if is_job(n + 3, EARLY + 3):
                    a_transpose(n + 3)
                if b < N_BLOCKS:
                    w_transpose("h", b)
                if not BHDMA and HS <= n < HS + 2:
                    spread_matmul("h", n - HS)
                if is_job(n + 1):
                    matmuls(n + 1, all_blocks)
                for o in (VX if n < N_TILES else VH):
                    if o == "e" and is_job(n):
                        bias_add(n, all_blocks)
                    if o == "q" and 1 <= b <= N_BLOCKS:
                        w_quantise("h", b - 1)
                    if o == "c" and is_job(n - CL, N_TILES):
                        combine(n - CL)
                    if o == "a" and is_job(n + 2, EARLY + 2):
                        a_quantise(n + 2)
                    if o == "r" and n + 3 in AV:
                        a_regroup(n + 3, True)
                    if o == "v":
                        if b < N_BLOCKS:
                            w_regroup("h", b, HV[b], True)
                        if not BHDMA and HS <= n < HS + 2:
                            spread_copy("h", n - HS)
                for o in (SX if n < N_TILES else SH):
                    if o == "d" and is_job(n - 1):
                        deviation(n - 1)
                    if o == "f" and BATCH <= n < BATCH + N_TILES and n % BATCH < len(X_STAGES):
                        x_factors((n // BATCH - 1) * BATCH, n % BATCH)
                    if o == "t":
                        if is_job(n - 1, N_TILES):
                            relation(n - 1)
                            shifts(n - 1)
                    if o == "a" and is_job(n + 3, EARLY + 3) and n + 3 not in AV:
                        a_regroup(n + 3)
                    if o == "m" and is_job(n):
                        mean(n)
                    if o == "w" and b < N_BLOCKS:
                        w_regroup("h", b, [c for c in range(4) if c not in HV[b]], False)
                    if o == "g" and is_job(n - GL, N_TILES):
                        gate(n - GL)
